import numpy as np
import ml_dtypes


def mxq(x, axis, fmt="e4m3"):
    dtype, down = {"e4m3": (ml_dtypes.float8_e4m3fn, 7), "e5m2": (ml_dtypes.float8_e5m2, 14)}[fmt]
    v = np.moveaxis(np.asarray(x, np.float32).astype(ml_dtypes.bfloat16).astype(np.float64), axis, -1)
    blocks = v.reshape(v.shape[:-1] + (-1, 32))
    amax = np.abs(blocks).max(-1, keepdims=True)
    byte = np.maximum(np.where(amax > 0, np.frexp(amax)[1] - 1 + 127, 0) - down, 1)
    scale = np.exp2(byte - 127.0)
    codes = (blocks / scale).astype(np.float32).astype(dtype).astype(np.float64)
    return np.moveaxis((codes * scale).reshape(v.shape), -1, axis)


WIDE = False


def mx_kscale(k):
    if not WIDE:
        return np.ones(k)
    levels = np.array([20, -20, 10, -10, 0])
    a = np.random.permutation(np.resize(levels, k // 512 * 4)).reshape(k // 512, 4)
    idx = np.arange(k)
    return np.exp2(a[idx // 512, idx % 128 // 32])


BF16 = ml_dtypes.bfloat16


def bf(x):
    return np.asarray(x, np.float32).astype(BF16)


def f64(x):
    return np.asarray(x).astype(np.float64)


Nc, Ns, Nt, d_h, BS = 64, 64, 16, 128, 16
I, J = Ns * Nt, Nc * Nt


def setup_inputs():
    u = mx_kscale(I)
    Ac = (np.random.random((Ns, Nc)) < 3.2 / Ns).astype(np.float64)
    Ac[np.random.randint(0, Ns, Nc), np.arange(Nc)] = 1.0
    Ac[np.arange(Ns), np.random.randint(0, Nc, Ns)] = 1.0
    As = (np.random.random((Ns, Ns)) < 0.05).astype(np.float64)
    AA = np.dot(np.dot(As, As), Ac) + np.dot(As, Ac) + Ac
    AA = (AA != 0).astype(np.float64)
    AA_mask = bf(np.tile(AA, (Nt, Nt)))
    g = 1.0 / np.sqrt(0.5 * J * AA.mean())
    GCW0 = bf(np.random.standard_normal((I, J)) * g)
    GCB = bf(np.random.standard_normal((I, d_h)) * 0.5)
    h = bf(np.random.standard_normal((BS, Nc, Nt, d_h)))
    e = bf(np.random.standard_normal(1) * 0.1)
    go = np.random.standard_normal((BS, Ns, Nt, d_h)) * np.exp2(np.random.randint(-12, 1, (BS, Ns, Nt, 1))) * 4.0
    A0 = np.maximum(f64(AA_mask) * f64(GCW0), 0.0)
    x0 = np.transpose(f64(h), (0, 2, 1, 3)).reshape(BS, J, d_h)
    z = A0 @ x0 + f64(GCB)
    zo = np.transpose(z.reshape(BS, Nt, Ns, d_h), (0, 2, 1, 3))
    go = go * (np.abs(zo) > 1e-4)
    go = go * u.reshape(Nt, Ns).T[None, :, :, None]
    GCW = bf(f64(GCW0) / u[:, None])
    return {"h": h, "e": e, "AA_mask": AA_mask, "GCW": GCW, "GCB": GCB, "z": np.asarray(z, np.float32), "grad_out": bf(go)}


def reference(h, e, AA_mask, GCW, GCB, z, grad_out):
    bs = grad_out.shape[0]
    A = np.maximum(f64(AA_mask) * f64(GCW), 0.0)
    g = np.transpose(f64(grad_out), (0, 2, 1, 3)).reshape(bs, I, d_h)
    dz = g * (f64(z) > 0.0)
    dzm = np.transpose(dz, (1, 0, 2)).reshape(I, bs * d_h)
    gx = mxq(A, 0, "e4m3").T @ mxq(dzm, 0, "e5m2")
    gx = gx.reshape(Nt, Nc, bs, d_h)
    return np.transpose(gx, (2, 1, 0, 3))

@@ -1,0 +1,120 @@
+from contextlib import ExitStack
+
+import concourse.mybir as mybir
+
+F32 = mybir.dt.float32
+BF16 = mybir.dt.bfloat16
+U32 = mybir.dt.uint32
+U8 = mybir.dt.uint8
+E4M3_X4 = mybir.dt.float8_e4m3fn_x4
+E5M2_X4 = mybir.dt.float8_e5m2_x4
+ALU = mybir.AluOpType
+
+P = 128
+PACK = 4
+K_PASS = P * PACK
+
+BATCH, NODES, STEPS, FEAT = 16, 64, 16, 128
+I = STEPS * NODES
+J = STEPS * NODES
+PASSES = I // K_PASS
+ROWS = I // P
+
+N_TILE = 512
+GROUP = N_TILE // FEAT
+GROUPS = BATCH // GROUP
+M_TILES = J // P
+HALF_STEPS = STEPS // 2
+
+FLOPS = 2 * I * J * BATCH * FEAT
+BYTES = 2 * (2 * I * J) + 4 * BATCH * I * FEAT + 2 * BATCH * I * FEAT + 4 * BATCH * J * FEAT
+
+
+def tile_gcnfast_t_v_kernel(tc, h, e, AA_mask, GCW, GCB, z, grad_out, out):
+    nc = tc.nc
+
+    mask_rows = AA_mask.rearrange("(g u p) j -> g p u j", u=PACK, p=P)
+    gcw_rows = GCW.rearrange("(g u p) j -> g p u j", u=PACK, p=P)
+    z_rows = z.rearrange("b (v p) d -> b p v d", p=P)
+    g_rows = grad_out.rearrange("b s (v half) d -> b half s v d", half=2)
+    out_rows = out.rearrange("b c t d -> b (c t d)").rearrange("b (q r) -> q b r", q=P)
+
+    with ExitStack() as ctx:
+        keep = ctx.enter_context(tc.tile_pool(name="keep", bufs=1))
+        weights = ctx.enter_context(tc.tile_pool(name="weights", bufs=2))
+        loads = ctx.enter_context(tc.tile_pool(name="loads", bufs=12))
+        quant = ctx.enter_context(tc.tile_pool(name="quant", bufs=2))
+        stores = ctx.enter_context(tc.tile_pool(name="stores", bufs=2))
+        psum = ctx.enter_context(tc.psum_pool(name="psum", bufs=8))
+
+        a_grouped = keep.tile([P, PASSES, J * PACK], BF16, align_bytes=64)
+        a_codes = keep.tile([P, PASSES, J], U32, align_bytes=64)
+        a_scales = keep.tile([P, PASSES, J], U8, align_bytes=64)
+        for g in range(PASSES):
+            mask_t = weights.tile([P, PACK, J], BF16)
+            gcw_t = weights.tile([P, PACK, J], BF16)
+            nc.sync.dma_start(out=mask_t[:], in_=mask_rows[g])
+            nc.sync.dma_start(out=gcw_t[:], in_=gcw_rows[g])
+            product = weights.tile([P, PACK, J], BF16)
+            nc.vector.tensor_tensor(out=product[:], in0=mask_t[:], in1=gcw_t[:], op=ALU.mult)
+            nc.vector.tensor_scalar_max(
+                out=a_grouped[:, g, :].rearrange("p (mc th u) -> p mc th u", th=2, u=PACK),
+                in0=product[:].rearrange("p u (th mc) -> p mc th u", th=2),
+                scalar1=0.0,
+            )
+            nc.vector.quantize_mx(
+                out=a_codes[:, g, :].bitcast(E4M3_X4),
+                scales=a_scales[:, g, :],
+                in_=a_grouped[:, g, :],
+            )
+
+        for group in range(GROUPS):
+            dz_grouped = quant.tile([P, PASSES, GROUP, FEAT, PACK], BF16, align_bytes=64)
+            for bl in range(GROUP):
+                b = group * GROUP + bl
+                g_t = loads.tile([P, ROWS, FEAT], BF16)
+                z_t = loads.tile([P, ROWS, FEAT], F32)
+                for half in range(2):
+                    nc.sync.dma_start(
+                        out=g_t[half * NODES : (half + 1) * NODES], in_=g_rows[b, half]
+                    )
+                nc.sync.dma_start(out=z_t[:], in_=z_rows[b])
+                for g in range(PASSES):
+                    rows = slice(g * PACK, (g + 1) * PACK)
+                    nc.vector.scalar_tensor_tensor(
+                        out=dz_grouped[:, g, bl, :, :],
+                        in0=z_t[:, rows, :].rearrange("p u d -> p d u"),
+                        scalar=0.0,
+                        in1=g_t[:, rows, :].rearrange("p u d -> p d u"),
+                        op0=ALU.is_gt,
+                        op1=ALU.mult,
+                    )
+            dz_codes = quant.tile([P, PASSES, N_TILE], U32, align_bytes=64)
+            dz_scales = quant.tile([P, PASSES, N_TILE], U8, align_bytes=64)
+            nc.vector.quantize_mx(
+                out=dz_codes[:].rearrange("p g n -> p (g n)").bitcast(E5M2_X4),
+                scales=dz_scales[:].rearrange("p g n -> p (g n)"),
+                in_=dz_grouped[:].rearrange("p g b d u -> p (g b d u)"),
+            )
+
+            staged = stores.tile([P, GROUP, HALF_STEPS, FEAT], F32)
+            for m in range(M_TILES):
+                cols = slice(m * P, (m + 1) * P)
+                acc = psum.tile([P, N_TILE], F32)
+                for g in range(PASSES):
+                    nc.tensor.matmul_mx(
+                        out=acc[:],
+                        lhsT=a_codes[:, g, cols].bitcast(E4M3_X4),
+                        lhsT_scale=a_scales[:, g, cols],
+                        rhs=dz_codes[:, g, :].bitcast(E5M2_X4),
+                        rhs_scale=dz_scales[:, g, :],
+                        start=(g == 0),
+                        stop=(g == PASSES - 1),
+                    )
+                nc.scalar.copy(
+                    out=staged[:, :, m, :], in_=acc[:].rearrange("p (b d) -> p b d", b=GROUP)
+                )
+            nc.scalar.dma_start(
+                out=out_rows[:, group * GROUP : (group + 1) * GROUP, :],
+                in_=staged[:].rearrange("p b t d -> p b (t d)"),
+            )

@@ -79,16 +79,19 @@ def tile_gcnfast_t_v_kernel(tc, h, e, AA_mask, GCW, GCB, z, grad_out, out):
                         out=g_t[half * NODES : (half + 1) * NODES], in_=g_rows[b, half]
                     )
                 nc.sync.dma_start(out=z_t[:], in_=z_rows[b])
-                for g in range(PASSES):
-                    rows = slice(g * PACK, (g + 1) * PACK)
-                    nc.vector.scalar_tensor_tensor(
-                        out=dz_grouped[:, g, bl, :, :],
-                        in0=z_t[:, rows, :].rearrange("p u d -> p d u"),
-                        scalar=0.0,
-                        in1=g_t[:, rows, :].rearrange("p u d -> p d u"),
-                        op0=ALU.is_gt,
-                        op1=ALU.mult,
-                    )
+                dz_rows = quant.tile([P, ROWS, FEAT], BF16, bufs=4)
+                nc.vector.scalar_tensor_tensor(
+                    out=dz_rows[:].rearrange("p v d -> p (v d)"),
+                    in0=z_t[:].rearrange("p v d -> p (v d)"),
+                    scalar=0.0,
+                    in1=g_t[:].rearrange("p v d -> p (v d)"),
+                    op0=ALU.is_gt,
+                    op1=ALU.mult,
+                )
+                nc.vector.tensor_copy(
+                    out=dz_grouped[:, :, bl, :, :],
+                    in_=dz_rows[:].rearrange("p (g u) d -> p g d u", u=PACK),
+                )
             dz_codes = quant.tile([P, PASSES, N_TILE], U32, align_bytes=64)
             dz_scales = quant.tile([P, PASSES, N_TILE], U8, align_bytes=64)
             nc.vector.quantize_mx(

@@ -36,32 +36,52 @@ def tile_gcnfast_t_v_kernel(tc, h, e, AA_mask, GCW, GCB, z, grad_out, out):
     mask_rows = AA_mask.rearrange("(g u p) j -> g p u j", u=PACK, p=P)
     gcw_rows = GCW.rearrange("(g u p) j -> g p u j", u=PACK, p=P)
     z_rows = z.rearrange("b (v p) d -> b p v d", p=P)
-    g_rows = grad_out.rearrange("b s (v half) d -> b half s v d", half=2)
+    g_rows = grad_out.rearrange("b s (v half) d -> v half s b d", half=2)
     out_rows = out.rearrange("b c t d -> b (c t d)").rearrange("b (q r) -> q b r", q=P)
 
     with ExitStack() as ctx:
         keep = ctx.enter_context(tc.tile_pool(name="keep", bufs=1))
-        weights = ctx.enter_context(tc.tile_pool(name="weights", bufs=2))
-        loads = ctx.enter_context(tc.tile_pool(name="loads", bufs=12))
+        weights = ctx.enter_context(tc.tile_pool(name="weights", bufs=PASSES))
+        loads = ctx.enter_context(tc.tile_pool(name="loads", bufs=3 * GROUP))
         quant = ctx.enter_context(tc.tile_pool(name="quant", bufs=2))
-        stores = ctx.enter_context(tc.tile_pool(name="stores", bufs=2))
+        stores = ctx.enter_context(tc.tile_pool(name="stores", bufs=3))
         psum = ctx.enter_context(tc.psum_pool(name="psum", bufs=8))
+        ctx.enter_context(tc.manual_schedule())
 
-        a_grouped = keep.tile([P, PASSES, J * PACK], BF16, align_bytes=64)
-        a_codes = keep.tile([P, PASSES, J], U32, align_bytes=64)
-        a_scales = keep.tile([P, PASSES, J], U8, align_bytes=64)
+        mask_tiles = []
+        gcw_tiles = []
         for g in range(PASSES):
             mask_t = weights.tile([P, PACK, J], BF16)
             gcw_t = weights.tile([P, PACK, J], BF16)
             nc.sync.dma_start(out=mask_t[:], in_=mask_rows[g])
             nc.sync.dma_start(out=gcw_t[:], in_=gcw_rows[g])
-            product = weights.tile([P, PACK, J], BF16)
-            nc.vector.tensor_tensor(out=product[:], in0=mask_t[:], in1=gcw_t[:], op=ALU.mult)
+            mask_tiles.append(mask_t)
+            gcw_tiles.append(gcw_t)
+        g_all = keep.tile([P, BATCH, ROWS, FEAT], BF16)
+        for v in range(ROWS):
+            for half in range(2):
+                nc.sync.dma_start(
+                    out=g_all[half * NODES : (half + 1) * NODES, :, v, :], in_=g_rows[v, half]
+                )
+        z_tiles = []
+        for b in range(BATCH):
+            z_t = loads.tile([P, ROWS, FEAT], F32)
+            nc.sync.dma_start(out=z_t[:], in_=z_rows[b])
+            z_tiles.append(z_t)
+
+        a_grouped = keep.tile([P, PASSES, J * PACK], BF16, align_bytes=64)
+        a_codes = keep.tile([P, PASSES, J], U32, align_bytes=64)
+        a_scales = keep.tile([P, PASSES, J], U8, align_bytes=64)
+        for g in range(PASSES):
+            nc.vector.tensor_tensor(
+                out=gcw_tiles[g][:], in0=mask_tiles[g][:], in1=gcw_tiles[g][:], op=ALU.mult
+            )
             nc.vector.tensor_scalar_max(
                 out=a_grouped[:, g, :].rearrange("p (mc th u) -> p mc th u", th=2, u=PACK),
-                in0=product[:].rearrange("p u (th mc) -> p mc th u", th=2),
+                in0=gcw_tiles[g][:].rearrange("p u (th mc) -> p mc th u", th=2),
                 scalar1=0.0,
             )
+        for g in range(PASSES):
             nc.vector.quantize_mx(
                 out=a_codes[:, g, :].bitcast(E4M3_X4),
                 scales=a_scales[:, g, :],
@@ -72,26 +92,16 @@ def tile_gcnfast_t_v_kernel(tc, h, e, AA_mask, GCW, GCB, z, grad_out, out):
             dz_grouped = quant.tile([P, PASSES, GROUP, FEAT, PACK], BF16, align_bytes=64)
             for bl in range(GROUP):
                 b = group * GROUP + bl
-                g_t = loads.tile([P, ROWS, FEAT], BF16)
-                z_t = loads.tile([P, ROWS, FEAT], F32)
-                for half in range(2):
-                    nc.sync.dma_start(
-                        out=g_t[half * NODES : (half + 1) * NODES], in_=g_rows[b, half]
+                for g in range(PASSES):
+                    rows = slice(g * PACK, (g + 1) * PACK)
+                    nc.vector.scalar_tensor_tensor(
+                        out=dz_grouped[:, g, bl, :, :],
+                        in0=z_tiles[b][:, rows, :].rearrange("p u d -> p d u"),
+                        scalar=0.0,
+                        in1=g_all[:, b, rows, :].rearrange("p u d -> p d u"),
+                        op0=ALU.is_gt,
+                        op1=ALU.mult,
                     )
-                nc.sync.dma_start(out=z_t[:], in_=z_rows[b])
-                dz_rows = quant.tile([P, ROWS, FEAT], BF16, bufs=4)
-                nc.vector.scalar_tensor_tensor(
-                    out=dz_rows[:].rearrange("p v d -> p (v d)"),
-                    in0=z_t[:].rearrange("p v d -> p (v d)"),
-                    scalar=0.0,
-                    in1=g_t[:].rearrange("p v d -> p (v d)"),
-                    op0=ALU.is_gt,
-                    op1=ALU.mult,
-                )
-                nc.vector.tensor_copy(
-                    out=dz_grouped[:, :, bl, :, :],
-                    in_=dz_rows[:].rearrange("p (g u) d -> p g d u", u=PACK),
-                )
             dz_codes = quant.tile([P, PASSES, N_TILE], U32, align_bytes=64)
             dz_scales = quant.tile([P, PASSES, N_TILE], U8, align_bytes=64)
             nc.vector.quantize_mx(
@@ -117,7 +127,7 @@ def tile_gcnfast_t_v_kernel(tc, h, e, AA_mask, GCW, GCB, z, grad_out, out):
                 nc.scalar.copy(
                     out=staged[:, :, m, :], in_=acc[:].rearrange("p (b d) -> p b d", b=GROUP)
                 )
-            nc.scalar.dma_start(
+            nc.sync.dma_start(
                 out=out_rows[:, group * GROUP : (group + 1) * GROUP, :],
                 in_=staged[:].rearrange("p b t d -> p b (t d)"),
             )

@@ -18,13 +18,15 @@ BATCH, NODES, STEPS, FEAT = 16, 64, 16, 128
 I = STEPS * NODES
 J = STEPS * NODES
 PASSES = I // K_PASS
-ROWS = I // P
+PARITIES = 2
+R = P // PARITIES
 
 N_TILE = 512
 GROUP = N_TILE // FEAT
 GROUPS = BATCH // GROUP
 M_TILES = J // P
 HALF_STEPS = STEPS // 2
+PAIR = 2
 
 FLOPS = 2 * I * J * BATCH * FEAT
 BYTES = 2 * (2 * I * J) + 4 * BATCH * I * FEAT + 2 * BATCH * I * FEAT + 4 * BATCH * J * FEAT
@@ -33,16 +35,18 @@ BYTES = 2 * (2 * I * J) + 4 * BATCH * I * FEAT + 2 * BATCH * I * FEAT + 4 * BATC
 def tile_gcnfast_t_v_kernel(tc, h, e, AA_mask, GCW, GCB, z, grad_out, out):
     nc = tc.nc
 
-    mask_rows = AA_mask.rearrange("(g u p) j -> g p u j", u=PACK, p=P)
-    gcw_rows = GCW.rearrange("(g u p) j -> g p u j", u=PACK, p=P)
-    z_rows = z.rearrange("b (v p) d -> b p v d", p=P)
-    g_rows = grad_out.rearrange("b s (v half) d -> v half s b d", half=2)
+    mask_rows = AA_mask.rearrange("(g e r u) j -> g e r (u j)", g=PASSES, e=PARITIES, u=PACK)
+    gcw_rows = GCW.rearrange("(g e r u) j -> g e r (u j)", g=PASSES, e=PARITIES, u=PACK)
+    z_rows = z.rearrange("b (g e r u) d -> e r (b g) (u d)", g=PASSES, e=PARITIES, u=PACK)
+    g_rows = grad_out.rearrange(
+        "b (s4 u) (g e tq) d -> g e tq u s4 b d", u=PACK, g=PASSES, e=PARITIES
+    )
     out_rows = out.rearrange("b c t d -> b (c t d)").rearrange("b (q r) -> q b r", q=P)
 
     with ExitStack() as ctx:
         keep = ctx.enter_context(tc.tile_pool(name="keep", bufs=1))
         weights = ctx.enter_context(tc.tile_pool(name="weights", bufs=PASSES))
-        loads = ctx.enter_context(tc.tile_pool(name="loads", bufs=3 * GROUP))
+        loads = ctx.enter_context(tc.tile_pool(name="loads", bufs=6))
         quant = ctx.enter_context(tc.tile_pool(name="quant", bufs=2))
         stores = ctx.enter_context(tc.tile_pool(name="stores", bufs=3))
         psum = ctx.enter_context(tc.psum_pool(name="psum", bufs=8))
@@ -53,20 +57,35 @@ def tile_gcnfast_t_v_kernel(tc, h, e, AA_mask, GCW, GCB, z, grad_out, out):
         for g in range(PASSES):
             mask_t = weights.tile([P, PACK, J], BF16)
             gcw_t = weights.tile([P, PACK, J], BF16)
-            nc.sync.dma_start(out=mask_t[:], in_=mask_rows[g])
-            nc.sync.dma_start(out=gcw_t[:], in_=gcw_rows[g])
+            for par in range(PARITIES):
+                nc.sync.dma_start(
+                    out=mask_t[par:P:PARITIES].rearrange("r u j -> r (u j)"),
+                    in_=mask_rows[g, par],
+                )
+                nc.sync.dma_start(
+                    out=gcw_t[par:P:PARITIES].rearrange("r u j -> r (u j)"),
+                    in_=gcw_rows[g, par],
+                )
             mask_tiles.append(mask_t)
             gcw_tiles.append(gcw_t)
-        g_all = keep.tile([P, BATCH, ROWS, FEAT], BF16)
-        for v in range(ROWS):
-            for half in range(2):
-                nc.sync.dma_start(
-                    out=g_all[half * NODES : (half + 1) * NODES, :, v, :], in_=g_rows[v, half]
-                )
+        g_all = keep.tile([P, BATCH, PASSES, PACK, FEAT], BF16)
+        for g in range(PASSES):
+            for par in range(PARITIES):
+                for tq in range(STEPS // (PASSES * PARITIES)):
+                    block = 32 * tq
+                    for u in range(PACK):
+                        nc.sync.dma_start(
+                            out=g_all[block + par : block + 32 : PARITIES, :, g, u, :],
+                            in_=g_rows[g, par, tq, u],
+                        )
         z_tiles = []
-        for b in range(BATCH):
-            z_t = loads.tile([P, ROWS, FEAT], F32)
-            nc.sync.dma_start(out=z_t[:], in_=z_rows[b])
+        for pair in range(BATCH // PAIR):
+            z_t = loads.tile([P, PAIR, PASSES, PACK, FEAT], F32)
+            for par in range(PARITIES):
+                nc.sync.dma_start(
+                    out=z_t[par:P:PARITIES].rearrange("r b g u d -> r (b g) (u d)"),
+                    in_=z_rows[par][:, pair * PAIR * PASSES : (pair + 1) * PAIR * PASSES, :],
+                )
             z_tiles.append(z_t)
 
         a_grouped = keep.tile([P, PASSES, J * PACK], BF16, align_bytes=64)
@@ -93,12 +112,11 @@ def tile_gcnfast_t_v_kernel(tc, h, e, AA_mask, GCW, GCB, z, grad_out, out):
             for bl in range(GROUP):
                 b = group * GROUP + bl
                 for g in range(PASSES):
-                    rows = slice(g * PACK, (g + 1) * PACK)
                     nc.vector.scalar_tensor_tensor(
                         out=dz_grouped[:, g, bl, :, :],
-                        in0=z_tiles[b][:, rows, :].rearrange("p u d -> p d u"),
+                        in0=z_tiles[b // PAIR][:, b % PAIR, g, :, :].rearrange("p u d -> p d u"),
                         scalar=0.0,
-                        in1=g_all[:, b, rows, :].rearrange("p u d -> p d u"),
+                        in1=g_all[:, b, g, :, :].rearrange("p u d -> p d u"),
                         op0=ALU.is_gt,
                         op1=ALU.mult,
                     )

@@ -26,7 +26,6 @@ GROUP = N_TILE // FEAT
 GROUPS = BATCH // GROUP
 M_TILES = J // P
 HALF_STEPS = STEPS // 2
-PAIR = 2
 
 FLOPS = 2 * I * J * BATCH * FEAT
 BYTES = 2 * (2 * I * J) + 4 * BATCH * I * FEAT + 2 * BATCH * I * FEAT + 4 * BATCH * J * FEAT
@@ -37,7 +36,7 @@ def tile_gcnfast_t_v_kernel(tc, h, e, AA_mask, GCW, GCB, z, grad_out, out):
 
     mask_rows = AA_mask.rearrange("(g e r u) j -> g e r (u j)", g=PASSES, e=PARITIES, u=PACK)
     gcw_rows = GCW.rearrange("(g e r u) j -> g e r (u j)", g=PASSES, e=PARITIES, u=PACK)
-    z_rows = z.rearrange("b (g e r u) d -> e r (b g) (u d)", g=PASSES, e=PARITIES, u=PACK)
+    z_rows = z.rearrange("b (g e r u) d -> g e r b (u d)", g=PASSES, e=PARITIES, u=PACK)
     g_rows = grad_out.rearrange(
         "b (s4 u) (g e tq) d -> g e tq u s4 b d", u=PACK, g=PASSES, e=PARITIES
     )
@@ -46,8 +45,8 @@ def tile_gcnfast_t_v_kernel(tc, h, e, AA_mask, GCW, GCB, z, grad_out, out):
     with ExitStack() as ctx:
         keep = ctx.enter_context(tc.tile_pool(name="keep", bufs=1))
         weights = ctx.enter_context(tc.tile_pool(name="weights", bufs=PASSES))
-        loads = ctx.enter_context(tc.tile_pool(name="loads", bufs=6))
-        quant = ctx.enter_context(tc.tile_pool(name="quant", bufs=2))
+        loads = ctx.enter_context(tc.tile_pool(name="loads", bufs=5))
+        quant = ctx.enter_context(tc.tile_pool(name="quant", bufs=3))
         stores = ctx.enter_context(tc.tile_pool(name="stores", bufs=3))
         psum = ctx.enter_context(tc.psum_pool(name="psum", bufs=8))
         ctx.enter_context(tc.manual_schedule())
@@ -68,25 +67,25 @@ def tile_gcnfast_t_v_kernel(tc, h, e, AA_mask, GCW, GCB, z, grad_out, out):
                 )
             mask_tiles.append(mask_t)
             gcw_tiles.append(gcw_t)
-        g_all = keep.tile([P, BATCH, PASSES, PACK, FEAT], BF16)
+        g_all = keep.tile([P, PASSES, BATCH, PACK, FEAT], BF16)
+        z_tiles = []
         for g in range(PASSES):
             for par in range(PARITIES):
                 for tq in range(STEPS // (PASSES * PARITIES)):
                     block = 32 * tq
                     for u in range(PACK):
                         nc.sync.dma_start(
-                            out=g_all[block + par : block + 32 : PARITIES, :, g, u, :],
+                            out=g_all[block + par : block + 32 : PARITIES, g, :, u, :],
                             in_=g_rows[g, par, tq, u],
                         )
-        z_tiles = []
-        for pair in range(BATCH // PAIR):
-            z_t = loads.tile([P, PAIR, PASSES, PACK, FEAT], F32)
-            for par in range(PARITIES):
-                nc.sync.dma_start(
-                    out=z_t[par:P:PARITIES].rearrange("r b g u d -> r (b g) (u d)"),
-                    in_=z_rows[par][:, pair * PAIR * PASSES : (pair + 1) * PAIR * PASSES, :],
-                )
-            z_tiles.append(z_t)
+            for group in range(GROUPS):
+                z_t = loads.tile([P, GROUP, PACK, FEAT], F32)
+                for par in range(PARITIES):
+                    nc.sync.dma_start(
+                        out=z_t[par:P:PARITIES].rearrange("r b u d -> r b (u d)"),
+                        in_=z_rows[g, par][:, group * GROUP : (group + 1) * GROUP, :],
+                    )
+                z_tiles.append(z_t)
 
         a_grouped = keep.tile([P, PASSES, J * PACK], BF16, align_bytes=64)
         a_codes = keep.tile([P, PASSES, J], U32, align_bytes=64)
@@ -107,27 +106,28 @@ def tile_gcnfast_t_v_kernel(tc, h, e, AA_mask, GCW, GCB, z, grad_out, out):
                 in_=a_grouped[:, g, :],
             )
 
-        for group in range(GROUPS):
-            dz_grouped = quant.tile([P, PASSES, GROUP, FEAT, PACK], BF16, align_bytes=64)
+        dz_codes = keep.tile([P, PASSES, GROUPS, N_TILE], U32, align_bytes=64)
+        dz_scales = keep.tile([P, PASSES, GROUPS, N_TILE], U8, align_bytes=64)
+
+        def quantise_dz(g, group):
+            z_t = z_tiles[g * GROUPS + group]
+            dz_grouped = quant.tile([P, GROUP, FEAT, PACK], BF16, align_bytes=64)
             for bl in range(GROUP):
-                b = group * GROUP + bl
-                for g in range(PASSES):
-                    nc.vector.scalar_tensor_tensor(
-                        out=dz_grouped[:, g, bl, :, :],
-                        in0=z_tiles[b // PAIR][:, b % PAIR, g, :, :].rearrange("p u d -> p d u"),
-                        scalar=0.0,
-                        in1=g_all[:, b, g, :, :].rearrange("p u d -> p d u"),
-                        op0=ALU.is_gt,
-                        op1=ALU.mult,
-                    )
-            dz_codes = quant.tile([P, PASSES, N_TILE], U32, align_bytes=64)
-            dz_scales = quant.tile([P, PASSES, N_TILE], U8, align_bytes=64)
+                nc.vector.scalar_tensor_tensor(
+                    out=dz_grouped[:, bl, :, :],
+                    in0=z_t[:, bl, :, :].rearrange("p u d -> p d u"),
+                    scalar=0.0,
+                    in1=g_all[:, g, group * GROUP + bl, :, :].rearrange("p u d -> p d u"),
+                    op0=ALU.is_gt,
+                    op1=ALU.mult,
+                )
             nc.vector.quantize_mx(
-                out=dz_codes[:].rearrange("p g n -> p (g n)").bitcast(E5M2_X4),
-                scales=dz_scales[:].rearrange("p g n -> p (g n)"),
-                in_=dz_grouped[:].rearrange("p g b d u -> p (g b d u)"),
+                out=dz_codes[:, g, group, :].bitcast(E5M2_X4),
+                scales=dz_scales[:, g, group, :],
+                in_=dz_grouped[:].rearrange("p b d u -> p (b d u)"),
             )
 
+        def multiply(group):
             staged = stores.tile([P, GROUP, HALF_STEPS, FEAT], F32)
             for m in range(M_TILES):
                 cols = slice(m * P, (m + 1) * P)
@@ -137,8 +137,8 @@ def tile_gcnfast_t_v_kernel(tc, h, e, AA_mask, GCW, GCB, z, grad_out, out):
                         out=acc[:],
                         lhsT=a_codes[:, g, cols].bitcast(E4M3_X4),
                         lhsT_scale=a_scales[:, g, cols],
-                        rhs=dz_codes[:, g, :].bitcast(E5M2_X4),
-                        rhs_scale=dz_scales[:, g, :],
+                        rhs=dz_codes[:, g, group, :].bitcast(E5M2_X4),
+                        rhs_scale=dz_scales[:, g, group, :],
                         start=(g == 0),
                         stop=(g == PASSES - 1),
                     )
@@ -149,3 +149,10 @@ def tile_gcnfast_t_v_kernel(tc, h, e, AA_mask, GCW, GCB, z, grad_out, out):
                 out=out_rows[:, group * GROUP : (group + 1) * GROUP, :],
                 in_=staged[:].rearrange("p b t d -> p b (t d)"),
             )
+
+        for g in range(PASSES - 1):
+            for group in range(GROUPS):
+                quantise_dz(g, group)
+        for group in range(GROUPS):
+            quantise_dz(PASSES - 1, group)
+            multiply(group)

@@ -1,5 +1,6 @@
 from contextlib import ExitStack
 
+import concourse.masks as masks
 import concourse.mybir as mybir
 
 F32 = mybir.dt.float32
@@ -18,14 +19,17 @@ BATCH, NODES, STEPS, FEAT = 16, 64, 16, 128
 I = STEPS * NODES
 J = STEPS * NODES
 PASSES = I // K_PASS
-PARITIES = 2
-R = P // PARITIES
+ROWS = I // P
 
 N_TILE = 512
 GROUP = N_TILE // FEAT
 GROUPS = BATCH // GROUP
 M_TILES = J // P
 HALF_STEPS = STEPS // 2
+PAIR = P // NODES
+PAIRS = BATCH // PAIR
+QUAD = 4
+BANK_BF16 = 1024
 
 FLOPS = 2 * I * J * BATCH * FEAT
 BYTES = 2 * (2 * I * J) + 4 * BATCH * I * FEAT + 2 * BATCH * I * FEAT + 4 * BATCH * J * FEAT
@@ -34,100 +38,133 @@ BYTES = 2 * (2 * I * J) + 4 * BATCH * I * FEAT + 2 * BATCH * I * FEAT + 4 * BATC
 def tile_gcnfast_t_v_kernel(tc, h, e, AA_mask, GCW, GCB, z, grad_out, out):
     nc = tc.nc
 
-    mask_rows = AA_mask.rearrange("(g e r u) j -> g e r (u j)", g=PASSES, e=PARITIES, u=PACK)
-    gcw_rows = GCW.rearrange("(g e r u) j -> g e r (u j)", g=PASSES, e=PARITIES, u=PACK)
-    z_rows = z.rearrange("b (g e r u) d -> g e r b (u d)", g=PASSES, e=PARITIES, u=PACK)
-    g_rows = grad_out.rearrange(
-        "b (s4 u) (g e tq) d -> g e tq u s4 b d", u=PACK, g=PASSES, e=PARITIES
-    )
+    mask_rows = AA_mask.rearrange("(g u p) j -> g p u j", u=PACK, p=P)
+    gcw_rows = GCW.rearrange("(g u p) j -> g p u j", u=PACK, p=P)
+    z_rows = z.rearrange("b (v p) d -> b p v d", p=P)
+    g_pairs = grad_out.rearrange("(pair bl) s t d -> pair (bl s) t d", bl=PAIR)
     out_rows = out.rearrange("b c t d -> b (c t d)").rearrange("b (q r) -> q b r", q=P)
 
     with ExitStack() as ctx:
         keep = ctx.enter_context(tc.tile_pool(name="keep", bufs=1))
-        weights = ctx.enter_context(tc.tile_pool(name="weights", bufs=PASSES))
-        loads = ctx.enter_context(tc.tile_pool(name="loads", bufs=5))
-        quant = ctx.enter_context(tc.tile_pool(name="quant", bufs=3))
-        stores = ctx.enter_context(tc.tile_pool(name="stores", bufs=3))
-        psum = ctx.enter_context(tc.psum_pool(name="psum", bufs=8))
+        loads = ctx.enter_context(tc.tile_pool(name="loads", bufs=3 * GROUP))
+        quant = ctx.enter_context(tc.tile_pool(name="quant", bufs=2))
         ctx.enter_context(tc.manual_schedule())
 
-        mask_tiles = []
-        gcw_tiles = []
-        for g in range(PASSES):
-            mask_t = weights.tile([P, PACK, J], BF16)
-            gcw_t = weights.tile([P, PACK, J], BF16)
-            for par in range(PARITIES):
-                nc.sync.dma_start(
-                    out=mask_t[par:P:PARITIES].rearrange("r u j -> r (u j)"),
-                    in_=mask_rows[g, par],
-                )
-                nc.sync.dma_start(
-                    out=gcw_t[par:P:PARITIES].rearrange("r u j -> r (u j)"),
-                    in_=gcw_rows[g, par],
-                )
-            mask_tiles.append(mask_t)
-            gcw_tiles.append(gcw_t)
-        g_all = keep.tile([P, PASSES, BATCH, PACK, FEAT], BF16)
-        z_tiles = []
-        for g in range(PASSES):
-            for par in range(PARITIES):
-                for tq in range(STEPS // (PASSES * PARITIES)):
-                    block = 32 * tq
-                    for u in range(PACK):
-                        nc.sync.dma_start(
-                            out=g_all[block + par : block + 32 : PARITIES, g, :, u, :],
-                            in_=g_rows[g, par, tq, u],
-                        )
-            for group in range(GROUPS):
-                z_t = loads.tile([P, GROUP, PACK, FEAT], F32)
-                for par in range(PARITIES):
-                    nc.sync.dma_start(
-                        out=z_t[par:P:PARITIES].rearrange("r b u d -> r b (u d)"),
-                        in_=z_rows[g, par][:, group * GROUP : (group + 1) * GROUP, :],
-                    )
-                z_tiles.append(z_t)
-
+        ident = keep.tile([P, P], BF16)
+        masks.make_identity(nc, ident[:])
         a_grouped = keep.tile([P, PASSES, J * PACK], BF16, align_bytes=64)
         a_codes = keep.tile([P, PASSES, J], U32, align_bytes=64)
         a_scales = keep.tile([P, PASSES, J], U8, align_bytes=64)
-        for g in range(PASSES):
-            nc.vector.tensor_tensor(
-                out=gcw_tiles[g][:], in0=mask_tiles[g][:], in1=gcw_tiles[g][:], op=ALU.mult
-            )
-            nc.vector.tensor_scalar_max(
-                out=a_grouped[:, g, :].rearrange("p (mc th u) -> p mc th u", th=2, u=PACK),
-                in0=gcw_tiles[g][:].rearrange("p u (th mc) -> p mc th u", th=2),
-                scalar1=0.0,
-            )
-        for g in range(PASSES):
-            nc.vector.quantize_mx(
-                out=a_codes[:, g, :].bitcast(E4M3_X4),
-                scales=a_scales[:, g, :],
-                in_=a_grouped[:, g, :],
-            )
+        g_all = keep.tile([P, BATCH, ROWS, FEAT], BF16)
 
-        dz_codes = keep.tile([P, PASSES, GROUPS, N_TILE], U32, align_bytes=64)
-        dz_scales = keep.tile([P, PASSES, GROUPS, N_TILE], U8, align_bytes=64)
+        with ExitStack() as head:
+            weights = head.enter_context(tc.tile_pool(name="weights", bufs=PASSES))
+            turn = head.enter_context(tc.tile_pool(name="turn", bufs=3))
+            turn_psum = head.enter_context(tc.psum_pool(name="turn_psum", bufs=4))
 
-        def quantise_dz(g, group):
-            z_t = z_tiles[g * GROUPS + group]
-            dz_grouped = quant.tile([P, GROUP, FEAT, PACK], BF16, align_bytes=64)
-            for bl in range(GROUP):
-                nc.vector.scalar_tensor_tensor(
-                    out=dz_grouped[:, bl, :, :],
-                    in0=z_t[:, bl, :, :].rearrange("p u d -> p d u"),
-                    scalar=0.0,
-                    in1=g_all[:, g, group * GROUP + bl, :, :].rearrange("p u d -> p d u"),
-                    op0=ALU.is_gt,
-                    op1=ALU.mult,
+            mask_tiles = []
+            gcw_tiles = []
+            for g in range(PASSES):
+                mask_t = weights.tile([P, PACK, J], BF16)
+                gcw_t = weights.tile([P, PACK, J], BF16)
+                nc.sync.dma_start(out=mask_t[:], in_=mask_rows[g])
+                nc.sync.dma_start(out=gcw_t[:], in_=gcw_rows[g])
+                mask_tiles.append(mask_t)
+                gcw_tiles.append(gcw_t)
+            g_tiles = []
+            for pair in range(PAIRS):
+                g_t = turn.tile([P, STEPS, FEAT], BF16, bufs=PAIRS)
+                nc.sync.dma_start(out=g_t[:], in_=g_pairs[pair])
+                g_tiles.append(g_t)
+            z_tiles = []
+            for b in range(BATCH):
+                z_t = loads.tile([P, ROWS, FEAT], F32)
+                nc.sync.dma_start(out=z_t[:], in_=z_rows[b])
+                z_tiles.append(z_t)
+
+            for g in range(PASSES):
+                nc.vector.tensor_tensor(
+                    out=gcw_tiles[g][:], in0=mask_tiles[g][:], in1=gcw_tiles[g][:], op=ALU.mult
                 )
+                nc.vector.tensor_scalar_max(
+                    out=a_grouped[:, g, :].rearrange("p (mc th u) -> p mc th u", th=2, u=PACK),
+                    in0=gcw_tiles[g][:].rearrange("p u (th mc) -> p mc th u", th=2),
+                    scalar1=0.0,
+                )
+            for g in range(PASSES):
+                nc.vector.quantize_mx(
+                    out=a_codes[:, g, :].bitcast(E4M3_X4),
+                    scales=a_scales[:, g, :],
+                    in_=a_grouped[:, g, :],
+                )
+
+            def turn_in(pair):
+                by_feature = turn.tile([P, PAIR, STEPS, NODES], BF16)
+                for quad in range(STEPS // QUAD):
+                    steps = slice(quad * QUAD, (quad + 1) * QUAD)
+                    bank_in = turn_psum.tile([P, BANK_BF16], BF16)
+                    for k in range(QUAD):
+                        nc.tensor.transpose(
+                            out=bank_in[:, k * P : (k + 1) * P],
+                            in_=g_tiles[pair][:, quad * QUAD + k, :],
+                            identity=ident[:],
+                        )
+                    nc.scalar.copy(
+                        out=by_feature[:, :, steps, :],
+                        in_=bank_in[:, : QUAD * P].rearrange(
+                            "d (t bl s) -> d bl t s", t=QUAD, bl=PAIR
+                        ),
+                    )
+                return by_feature
+
+            def turn_back(pair, by_feature):
+                for bl in range(PAIR):
+                    by_i = by_feature[:, bl, :, :].rearrange("d t s -> d (t s)")
+                    for quad in range(ROWS // QUAD):
+                        rows = slice(quad * QUAD, (quad + 1) * QUAD)
+                        bank_back = turn_psum.tile([P, BANK_BF16], BF16)
+                        for k in range(QUAD):
+                            v = quad * QUAD + k
+                            nc.tensor.transpose(
+                                out=bank_back[:, k * P : (k + 1) * P],
+                                in_=by_i[:, v * P : (v + 1) * P],
+                                identity=ident[:],
+                            )
+                        nc.scalar.copy(
+                            out=g_all[:, pair * PAIR + bl, rows, :],
+                            in_=bank_back[:, : QUAD * P].rearrange("p (v d) -> p v d", v=QUAD),
+                        )
+
+            by_feature = turn_in(0)
+            for pair in range(PAIRS):
+                following = turn_in(pair + 1) if pair + 1 < PAIRS else None
+                turn_back(pair, by_feature)
+                by_feature = following
+
+        stores = ctx.enter_context(tc.tile_pool(name="stores", bufs=3))
+        psum = ctx.enter_context(tc.psum_pool(name="psum", bufs=8))
+        for group in range(GROUPS):
+            dz_grouped = quant.tile([P, PASSES, GROUP, FEAT, PACK], BF16, align_bytes=64)
+            for bl in range(GROUP):
+                b = group * GROUP + bl
+                for g in range(PASSES):
+                    rows = slice(g * PACK, (g + 1) * PACK)
+                    nc.vector.scalar_tensor_tensor(
+                        out=dz_grouped[:, g, bl, :, :],
+                        in0=z_tiles[b][:, rows, :].rearrange("p u d -> p d u"),
+                        scalar=0.0,
+                        in1=g_all[:, b, rows, :].rearrange("p u d -> p d u"),
+                        op0=ALU.is_gt,
+                        op1=ALU.mult,
+                    )
+            dz_codes = quant.tile([P, PASSES, N_TILE], U32, align_bytes=64)
+            dz_scales = quant.tile([P, PASSES, N_TILE], U8, align_bytes=64)
             nc.vector.quantize_mx(
-                out=dz_codes[:, g, group, :].bitcast(E5M2_X4),
-                scales=dz_scales[:, g, group, :],
-                in_=dz_grouped[:].rearrange("p b d u -> p (b d u)"),
+                out=dz_codes[:].rearrange("p g n -> p (g n)").bitcast(E5M2_X4),
+                scales=dz_scales[:].rearrange("p g n -> p (g n)"),
+                in_=dz_grouped[:].rearrange("p g b d u -> p (g b d u)"),
             )
 
-        def multiply(group):
             staged = stores.tile([P, GROUP, HALF_STEPS, FEAT], F32)
             for m in range(M_TILES):
                 cols = slice(m * P, (m + 1) * P)
@@ -137,8 +174,8 @@ def tile_gcnfast_t_v_kernel(tc, h, e, AA_mask, GCW, GCB, z, grad_out, out):
                         out=acc[:],
                         lhsT=a_codes[:, g, cols].bitcast(E4M3_X4),
                         lhsT_scale=a_scales[:, g, cols],
-                        rhs=dz_codes[:, g, group, :].bitcast(E5M2_X4),
-                        rhs_scale=dz_scales[:, g, group, :],
+                        rhs=dz_codes[:, g, :].bitcast(E5M2_X4),
+                        rhs_scale=dz_scales[:, g, :],
                         start=(g == 0),
                         stop=(g == PASSES - 1),
                     )
@@ -149,10 +186,3 @@ def tile_gcnfast_t_v_kernel(tc, h, e, AA_mask, GCW, GCB, z, grad_out, out):
                 out=out_rows[:, group * GROUP : (group + 1) * GROUP, :],
                 in_=staged[:].rearrange("p b t d -> p b (t d)"),
             )
-
-        for g in range(PASSES - 1):
-            for group in range(GROUPS):
-                quantise_dz(g, group)
-        for group in range(GROUPS):
-            quantise_dz(PASSES - 1, group)
-            multiply(group)

@@ -30,6 +30,7 @@ PAIR = P // NODES
 PAIRS = BATCH // PAIR
 QUAD = 4
 BANK_BF16 = 1024
+TURN_BANKS = 4
 
 FLOPS = 2 * I * J * BATCH * FEAT
 BYTES = 2 * (2 * I * J) + 4 * BATCH * I * FEAT + 2 * BATCH * I * FEAT + 4 * BATCH * J * FEAT
@@ -48,6 +49,8 @@ def tile_gcnfast_t_v_kernel(tc, h, e, AA_mask, GCW, GCB, z, grad_out, out):
         keep = ctx.enter_context(tc.tile_pool(name="keep", bufs=1))
         loads = ctx.enter_context(tc.tile_pool(name="loads", bufs=3 * GROUP))
         quant = ctx.enter_context(tc.tile_pool(name="quant", bufs=2))
+        turn_psum = ctx.enter_context(tc.psum_pool(name="turn_psum", bufs=TURN_BANKS))
+        psum = ctx.enter_context(tc.psum_pool(name="psum", bufs=8 - TURN_BANKS))
         ctx.enter_context(tc.manual_schedule())
 
         ident = keep.tile([P, P], BF16)
@@ -55,12 +58,11 @@ def tile_gcnfast_t_v_kernel(tc, h, e, AA_mask, GCW, GCB, z, grad_out, out):
         a_grouped = keep.tile([P, PASSES, J * PACK], BF16, align_bytes=64)
         a_codes = keep.tile([P, PASSES, J], U32, align_bytes=64)
         a_scales = keep.tile([P, PASSES, J], U8, align_bytes=64)
-        g_all = keep.tile([P, BATCH, ROWS, FEAT], BF16)
+        by_feature = keep.tile([P, BATCH, STEPS, NODES], BF16)
 
         with ExitStack() as head:
             weights = head.enter_context(tc.tile_pool(name="weights", bufs=PASSES))
-            turn = head.enter_context(tc.tile_pool(name="turn", bufs=3))
-            turn_psum = head.enter_context(tc.psum_pool(name="turn_psum", bufs=4))
+            as_it_lies = head.enter_context(tc.tile_pool(name="as_it_lies", bufs=PAIRS))
 
             mask_tiles = []
             gcw_tiles = []
@@ -73,7 +75,7 @@ def tile_gcnfast_t_v_kernel(tc, h, e, AA_mask, GCW, GCB, z, grad_out, out):
                 gcw_tiles.append(gcw_t)
             g_tiles = []
             for pair in range(PAIRS):
-                g_t = turn.tile([P, STEPS, FEAT], BF16, bufs=PAIRS)
+                g_t = as_it_lies.tile([P, STEPS, FEAT], BF16)
                 nc.sync.dma_start(out=g_t[:], in_=g_pairs[pair])
                 g_tiles.append(g_t)
             z_tiles = []
@@ -98,11 +100,11 @@ def tile_gcnfast_t_v_kernel(tc, h, e, AA_mask, GCW, GCB, z, grad_out, out):
                     in_=a_grouped[:, g, :],
                 )
 
-            def turn_in(pair):
-                by_feature = turn.tile([P, PAIR, STEPS, NODES], BF16)
+            for pair in range(PAIRS):
+                batches = slice(pair * PAIR, (pair + 1) * PAIR)
                 for quad in range(STEPS // QUAD):
                     steps = slice(quad * QUAD, (quad + 1) * QUAD)
-                    bank_in = turn_psum.tile([P, BANK_BF16], BF16)
+                    bank_in = turn_psum.tile([P, BANK_BF16], BF16, tag="turn")
                     for k in range(QUAD):
                         nc.tensor.transpose(
                             out=bank_in[:, k * P : (k + 1) * P],
@@ -110,39 +112,25 @@ def tile_gcnfast_t_v_kernel(tc, h, e, AA_mask, GCW, GCB, z, grad_out, out):
                             identity=ident[:],
                         )
                     nc.scalar.copy(
-                        out=by_feature[:, :, steps, :],
+                        out=by_feature[:, batches, steps, :],
                         in_=bank_in[:, : QUAD * P].rearrange(
                             "d (t bl s) -> d bl t s", t=QUAD, bl=PAIR
                         ),
                     )
-                return by_feature
 
-            def turn_back(pair, by_feature):
-                for bl in range(PAIR):
-                    by_i = by_feature[:, bl, :, :].rearrange("d t s -> d (t s)")
-                    for quad in range(ROWS // QUAD):
-                        rows = slice(quad * QUAD, (quad + 1) * QUAD)
-                        bank_back = turn_psum.tile([P, BANK_BF16], BF16)
-                        for k in range(QUAD):
-                            v = quad * QUAD + k
-                            nc.tensor.transpose(
-                                out=bank_back[:, k * P : (k + 1) * P],
-                                in_=by_i[:, v * P : (v + 1) * P],
-                                identity=ident[:],
-                            )
-                        nc.scalar.copy(
-                            out=g_all[:, pair * PAIR + bl, rows, :],
-                            in_=bank_back[:, : QUAD * P].rearrange("p (v d) -> p v d", v=QUAD),
-                        )
-
-            by_feature = turn_in(0)
-            for pair in range(PAIRS):
-                following = turn_in(pair + 1) if pair + 1 < PAIRS else None
-                turn_back(pair, by_feature)
-                by_feature = following
+        def turn_back(b):
+            by_i = by_feature[:, b, :, :].rearrange("d t s -> d (t s)")
+            bank_back = turn_psum.tile([P, ROWS, FEAT], BF16, tag="turn")
+            for v in range(ROWS):
+                nc.tensor.transpose(
+                    out=bank_back[:, v, :], in_=by_i[:, v * P : (v + 1) * P], identity=ident[:]
+                )
+            return bank_back
 
         stores = ctx.enter_context(tc.tile_pool(name="stores", bufs=3))
-        psum = ctx.enter_context(tc.psum_pool(name="psum", bufs=8))
+        g_banks = []
+        for b in range(TURN_BANKS):
+            g_banks.append(turn_back(b))
         for group in range(GROUPS):
             dz_grouped = quant.tile([P, PASSES, GROUP, FEAT, PACK], BF16, align_bytes=64)
             for bl in range(GROUP):
@@ -153,10 +141,12 @@ def tile_gcnfast_t_v_kernel(tc, h, e, AA_mask, GCW, GCB, z, grad_out, out):
                         out=dz_grouped[:, g, bl, :, :],
                         in0=z_tiles[b][:, rows, :].rearrange("p u d -> p d u"),
                         scalar=0.0,
-                        in1=g_all[:, b, rows, :].rearrange("p u d -> p d u"),
+                        in1=g_banks[b][:, rows, :].rearrange("p u d -> p d u"),
                         op0=ALU.is_gt,
                         op1=ALU.mult,
                     )
+                if b + TURN_BANKS < BATCH:
+                    g_banks.append(turn_back(b + TURN_BANKS))
             dz_codes = quant.tile([P, PASSES, N_TILE], U32, align_bytes=64)
             dz_scales = quant.tile([P, PASSES, N_TILE], U8, align_bytes=64)
             nc.vector.quantize_mx(

@@ -20,6 +20,7 @@ I = STEPS * NODES
 J = STEPS * NODES
 PASSES = I // K_PASS
 ROWS = I // P
+QUARTETS = NODES // PACK
 
 N_TILE = 512
 GROUP = N_TILE // FEAT
@@ -39,15 +40,15 @@ BYTES = 2 * (2 * I * J) + 4 * BATCH * I * FEAT + 2 * BATCH * I * FEAT + 4 * BATC
 def tile_gcnfast_t_v_kernel(tc, h, e, AA_mask, GCW, GCB, z, grad_out, out):
     nc = tc.nc
 
-    mask_rows = AA_mask.rearrange("(g u p) j -> g p u j", u=PACK, p=P)
-    gcw_rows = GCW.rearrange("(g u p) j -> g p u j", u=PACK, p=P)
-    z_rows = z.rearrange("b (v p) d -> b p v d", p=P)
+    mask_rows = AA_mask.rearrange("(g p u) j -> g p (u j)", p=P, u=PACK)
+    gcw_rows = GCW.rearrange("(g p u) j -> g p (u j)", p=P, u=PACK)
+    z_rows = z.rearrange("b (g p u) d -> p (b g) (u d)", p=P, u=PACK)
     g_pairs = grad_out.rearrange("(pair bl) s t d -> pair (bl s) t d", bl=PAIR)
     out_rows = out.rearrange("b c t d -> b (c t d)").rearrange("b (q r) -> q b r", q=P)
 
     with ExitStack() as ctx:
         keep = ctx.enter_context(tc.tile_pool(name="keep", bufs=1))
-        loads = ctx.enter_context(tc.tile_pool(name="loads", bufs=3 * GROUP))
+        loads = ctx.enter_context(tc.tile_pool(name="loads", bufs=6))
         quant = ctx.enter_context(tc.tile_pool(name="quant", bufs=2))
         turn_psum = ctx.enter_context(tc.psum_pool(name="turn_psum", bufs=TURN_BANKS))
         psum = ctx.enter_context(tc.psum_pool(name="psum", bufs=8 - TURN_BANKS))
@@ -55,10 +56,15 @@ def tile_gcnfast_t_v_kernel(tc, h, e, AA_mask, GCW, GCB, z, grad_out, out):
 
         ident = keep.tile([P, P], BF16)
         masks.make_identity(nc, ident[:])
+        sorter = keep.tile([P, P], BF16)
+        nc.vector.tensor_copy(
+            out=sorter[:].rearrange("i (bl u s4) -> i bl u s4", bl=PAIR, u=PACK),
+            in_=ident[:].rearrange("i (bl s4 u) -> i bl u s4", bl=PAIR, u=PACK),
+        )
         a_grouped = keep.tile([P, PASSES, J * PACK], BF16, align_bytes=64)
         a_codes = keep.tile([P, PASSES, J], U32, align_bytes=64)
         a_scales = keep.tile([P, PASSES, J], U8, align_bytes=64)
-        by_feature = keep.tile([P, BATCH, STEPS, NODES], BF16)
+        by_feature = keep.tile([P, PASSES, BATCH, PACK, P], BF16)
 
         with ExitStack() as head:
             weights = head.enter_context(tc.tile_pool(name="weights", bufs=PASSES))
@@ -69,8 +75,8 @@ def tile_gcnfast_t_v_kernel(tc, h, e, AA_mask, GCW, GCB, z, grad_out, out):
             for g in range(PASSES):
                 mask_t = weights.tile([P, PACK, J], BF16)
                 gcw_t = weights.tile([P, PACK, J], BF16)
-                nc.sync.dma_start(out=mask_t[:], in_=mask_rows[g])
-                nc.sync.dma_start(out=gcw_t[:], in_=gcw_rows[g])
+                nc.sync.dma_start(out=mask_t[:].rearrange("p u j -> p (u j)"), in_=mask_rows[g])
+                nc.sync.dma_start(out=gcw_t[:].rearrange("p u j -> p (u j)"), in_=gcw_rows[g])
                 mask_tiles.append(mask_t)
                 gcw_tiles.append(gcw_t)
             g_tiles = []
@@ -79,9 +85,12 @@ def tile_gcnfast_t_v_kernel(tc, h, e, AA_mask, GCW, GCB, z, grad_out, out):
                 nc.sync.dma_start(out=g_t[:], in_=g_pairs[pair])
                 g_tiles.append(g_t)
             z_tiles = []
-            for b in range(BATCH):
-                z_t = loads.tile([P, ROWS, FEAT], F32)
-                nc.sync.dma_start(out=z_t[:], in_=z_rows[b])
+            for pair in range(PAIRS):
+                z_t = loads.tile([P, PAIR, ROWS, FEAT], F32)
+                nc.sync.dma_start(
+                    out=z_t[:].rearrange("p b (g u) d -> p (b g) (u d)", u=PACK),
+                    in_=z_rows[:, pair * PAIR * PASSES : (pair + 1) * PAIR * PASSES, :],
+                )
                 z_tiles.append(z_t)
 
             for g in range(PASSES):
@@ -103,28 +112,33 @@ def tile_gcnfast_t_v_kernel(tc, h, e, AA_mask, GCW, GCB, z, grad_out, out):
             for pair in range(PAIRS):
                 batches = slice(pair * PAIR, (pair + 1) * PAIR)
                 for quad in range(STEPS // QUAD):
-                    steps = slice(quad * QUAD, (quad + 1) * QUAD)
                     bank_in = turn_psum.tile([P, BANK_BF16], BF16, tag="turn")
                     for k in range(QUAD):
                         nc.tensor.transpose(
                             out=bank_in[:, k * P : (k + 1) * P],
                             in_=g_tiles[pair][:, quad * QUAD + k, :],
-                            identity=ident[:],
+                            identity=sorter[:],
                         )
+                    g = quad * QUAD // HALF_STEPS
+                    first_p = (quad * QUAD % HALF_STEPS) * QUARTETS
                     nc.scalar.copy(
-                        out=by_feature[:, batches, steps, :],
+                        out=by_feature[
+                            :, g, batches, :, first_p : first_p + QUAD * QUARTETS
+                        ].rearrange("d bl u (k s4) -> d (bl u) k s4", k=QUAD),
                         in_=bank_in[:, : QUAD * P].rearrange(
-                            "d (t bl s) -> d bl t s", t=QUAD, bl=PAIR
+                            "d (k blu s4) -> d blu k s4", k=QUAD, s4=QUARTETS
                         ),
                     )
 
         def turn_back(b):
-            by_i = by_feature[:, b, :, :].rearrange("d t s -> d (t s)")
             bank_back = turn_psum.tile([P, ROWS, FEAT], BF16, tag="turn")
-            for v in range(ROWS):
-                nc.tensor.transpose(
-                    out=bank_back[:, v, :], in_=by_i[:, v * P : (v + 1) * P], identity=ident[:]
-                )
+            for g in range(PASSES):
+                for u in range(PACK):
+                    nc.tensor.transpose(
+                        out=bank_back[:, g * PACK + u, :],
+                        in_=by_feature[:, g, b, u, :],
+                        identity=ident[:],
+                    )
             return bank_back
 
         stores = ctx.enter_context(tc.tile_pool(name="stores", bufs=3))
@@ -139,7 +153,7 @@ def tile_gcnfast_t_v_kernel(tc, h, e, AA_mask, GCW, GCB, z, grad_out, out):
                     rows = slice(g * PACK, (g + 1) * PACK)
                     nc.vector.scalar_tensor_tensor(
                         out=dz_grouped[:, g, bl, :, :],
-                        in0=z_tiles[b][:, rows, :].rearrange("p u d -> p d u"),
+                        in0=z_tiles[b // PAIR][:, b % PAIR, rows, :].rearrange("p u d -> p d u"),
                         scalar=0.0,
                         in1=g_banks[b][:, rows, :].rearrange("p u d -> p d u"),
                         op0=ALU.is_gt,

@@ -56,15 +56,17 @@ def tile_gcnfast_t_v_kernel(tc, h, e, AA_mask, GCW, GCB, z, grad_out, out):
 
         ident = keep.tile([P, P], BF16)
         masks.make_identity(nc, ident[:])
+        ident_words = keep.tile([P, P], F32)
+        masks.make_identity(nc, ident_words[:])
         sorter = keep.tile([P, P], BF16)
         nc.vector.tensor_copy(
-            out=sorter[:].rearrange("i (bl u s4) -> i bl u s4", bl=PAIR, u=PACK),
-            in_=ident[:].rearrange("i (bl s4 u) -> i bl u s4", bl=PAIR, u=PACK),
+            out=sorter[:].bitcast(F32).rearrange("i (bl u2 s4) -> i bl u2 s4", bl=PAIR, u2=2),
+            in_=ident[:].bitcast(F32).rearrange("i (bl s4 u2) -> i bl u2 s4", bl=PAIR, u2=2),
         )
         a_grouped = keep.tile([P, PASSES, J * PACK], BF16, align_bytes=64)
         a_codes = keep.tile([P, PASSES, J], U32, align_bytes=64)
         a_scales = keep.tile([P, PASSES, J], U8, align_bytes=64)
-        by_feature = keep.tile([P, PASSES, BATCH, PACK, P], BF16)
+        by_feature = keep.tile([P, PASSES, BATCH, 2, P, 2], BF16)
 
         with ExitStack() as head:
             weights = head.enter_context(tc.tile_pool(name="weights", bufs=PASSES))
@@ -122,22 +124,26 @@ def tile_gcnfast_t_v_kernel(tc, h, e, AA_mask, GCW, GCB, z, grad_out, out):
                     g = quad * QUAD // HALF_STEPS
                     first_p = (quad * QUAD % HALF_STEPS) * QUARTETS
                     nc.scalar.copy(
-                        out=by_feature[
-                            :, g, batches, :, first_p : first_p + QUAD * QUARTETS
-                        ].rearrange("d bl u (k s4) -> d (bl u) k s4", k=QUAD),
-                        in_=bank_in[:, : QUAD * P].rearrange(
-                            "d (k blu s4) -> d blu k s4", k=QUAD, s4=QUARTETS
-                        ),
+                        out=by_feature[:, g, batches, :, :, :]
+                        .rearrange("d bl u2 p e -> d (bl u2 p e)")
+                        .bitcast(F32)
+                        .rearrange("d (blu p) -> d blu p", p=P)[
+                            :, :, first_p : first_p + QUAD * QUARTETS
+                        ]
+                        .rearrange("d blu (k s4) -> d blu k s4", k=QUAD),
+                        in_=bank_in[:, : QUAD * P]
+                        .bitcast(F32)
+                        .rearrange("d (k blu s4) -> d blu k s4", k=QUAD, s4=QUARTETS),
                     )
 
         def turn_back(b):
-            bank_back = turn_psum.tile([P, ROWS, FEAT], BF16, tag="turn")
+            bank_back = turn_psum.tile([P, PASSES, FEAT, 2], F32, tag="turn")
             for g in range(PASSES):
-                for u in range(PACK):
+                for u2 in range(2):
                     nc.tensor.transpose(
-                        out=bank_back[:, g * PACK + u, :],
-                        in_=by_feature[:, g, b, u, :],
-                        identity=ident[:],
+                        out=bank_back[:, g, :, u2],
+                        in_=by_feature[:, g, b, u2, :, :].rearrange("d p e -> d (p e)").bitcast(F32),
+                        identity=ident_words[:],
                     )
             return bank_back
 
@@ -155,7 +161,10 @@ def tile_gcnfast_t_v_kernel(tc, h, e, AA_mask, GCW, GCB, z, grad_out, out):
                         out=dz_grouped[:, g, bl, :, :],
                         in0=z_tiles[b // PAIR][:, b % PAIR, rows, :].rearrange("p u d -> p d u"),
                         scalar=0.0,
-                        in1=g_banks[b][:, rows, :].rearrange("p u d -> p d u"),
+                        in1=g_banks[b][:, g, :, :]
+                        .rearrange("p d u2 -> p (d u2)")
+                        .bitcast(BF16)
+                        .rearrange("p (d u) -> p d u", u=PACK),
                         op0=ALU.is_gt,
                         op1=ALU.mult,
                     )

@@ -31,6 +31,7 @@ PAIR = P // NODES
 PAIRS = BATCH // PAIR
 QUAD = 4
 BANK_BF16 = 1024
+FIRST_PAIRS = 2
 TURN_BANKS = 4
 
 FLOPS = 2 * I * J * BATCH * FEAT
@@ -68,6 +69,19 @@ def tile_gcnfast_t_v_kernel(tc, h, e, AA_mask, GCW, GCB, z, grad_out, out):
         a_scales = keep.tile([P, PASSES, J], U8, align_bytes=64)
         by_feature = keep.tile([P, PASSES, BATCH, 2, P, 2], BF16)
 
+        def turn_back(b):
+            bank_back = turn_psum.tile([P, PASSES, FEAT, 2], F32, tag="turn")
+            for g in range(PASSES):
+                for u2 in range(2):
+                    nc.tensor.transpose(
+                        out=bank_back[:, g, :, u2],
+                        in_=by_feature[:, g, b, u2, :, :].rearrange("d p e -> d (p e)").bitcast(F32),
+                        identity=ident_words[:],
+                    )
+            return bank_back
+
+        g_banks = []
+
         with ExitStack() as head:
             weights = head.enter_context(tc.tile_pool(name="weights", bufs=PASSES))
             as_it_lies = head.enter_context(tc.tile_pool(name="as_it_lies", bufs=PAIRS))
@@ -82,18 +96,29 @@ def tile_gcnfast_t_v_kernel(tc, h, e, AA_mask, GCW, GCB, z, grad_out, out):
                 mask_tiles.append(mask_t)
                 gcw_tiles.append(gcw_t)
             g_tiles = []
-            for pair in range(PAIRS):
+            z_tiles = []
+
+            def load_g(pair):
                 g_t = as_it_lies.tile([P, STEPS, FEAT], BF16)
                 nc.sync.dma_start(out=g_t[:], in_=g_pairs[pair])
                 g_tiles.append(g_t)
-            z_tiles = []
-            for pair in range(PAIRS):
+
+            def load_z(pair):
                 z_t = loads.tile([P, PAIR, ROWS, FEAT], F32)
                 nc.sync.dma_start(
                     out=z_t[:].rearrange("p b (g u) d -> p (b g) (u d)", u=PACK),
                     in_=z_rows[:, pair * PAIR * PASSES : (pair + 1) * PAIR * PASSES, :],
                 )
                 z_tiles.append(z_t)
+
+            for pair in range(FIRST_PAIRS):
+                load_g(pair)
+            for pair in range(FIRST_PAIRS):
+                load_z(pair)
+            for pair in range(FIRST_PAIRS, PAIRS):
+                load_g(pair)
+            for pair in range(FIRST_PAIRS, PAIRS):
+                load_z(pair)
 
             for g in range(PASSES):
                 nc.vector.tensor_tensor(
@@ -114,7 +139,7 @@ def tile_gcnfast_t_v_kernel(tc, h, e, AA_mask, GCW, GCB, z, grad_out, out):
             for pair in range(PAIRS):
                 batches = slice(pair * PAIR, (pair + 1) * PAIR)
                 for quad in range(STEPS // QUAD):
-                    bank_in = turn_psum.tile([P, BANK_BF16], BF16, tag="turn")
+                    bank_in = psum.tile([P, BANK_BF16], BF16, tag="acc")
                     for k in range(QUAD):
                         nc.tensor.transpose(
                             out=bank_in[:, k * P : (k + 1) * P],
@@ -135,22 +160,11 @@ def tile_gcnfast_t_v_kernel(tc, h, e, AA_mask, GCW, GCB, z, grad_out, out):
                         .bitcast(F32)
                         .rearrange("d (k blu s4) -> d blu k s4", k=QUAD, s4=QUARTETS),
                     )
-
-        def turn_back(b):
-            bank_back = turn_psum.tile([P, PASSES, FEAT, 2], F32, tag="turn")
-            for g in range(PASSES):
-                for u2 in range(2):
-                    nc.tensor.transpose(
-                        out=bank_back[:, g, :, u2],
-                        in_=by_feature[:, g, b, u2, :, :].rearrange("d p e -> d (p e)").bitcast(F32),
-                        identity=ident_words[:],
-                    )
-            return bank_back
+                if pair == FIRST_PAIRS - 1:
+                    for b in range(TURN_BANKS):
+                        g_banks.append(turn_back(b))
 
         stores = ctx.enter_context(tc.tile_pool(name="stores", bufs=3))
-        g_banks = []
-        for b in range(TURN_BANKS):
-            g_banks.append(turn_back(b))
         for group in range(GROUPS):
             dz_grouped = quant.tile([P, PASSES, GROUP, FEAT, PACK], BF16, align_bytes=64)
             for bl in range(GROUP):
@@ -181,7 +195,7 @@ def tile_gcnfast_t_v_kernel(tc, h, e, AA_mask, GCW, GCB, z, grad_out, out):
             staged = stores.tile([P, GROUP, HALF_STEPS, FEAT], F32)
             for m in range(M_TILES):
                 cols = slice(m * P, (m + 1) * P)
-                acc = psum.tile([P, N_TILE], F32)
+                acc = psum.tile([P, N_TILE], F32, tag="acc")
                 for g in range(PASSES):
                     nc.tensor.matmul_mx(
                         out=acc[:],

@@ -31,6 +31,7 @@ PAIR = P // NODES
 PAIRS = BATCH // PAIR
 QUAD = 4
 BANK_BF16 = 1024
+LAST_PIECES = (4, 6, 8)
 FIRST_PAIRS = 2
 TURN_BANKS = 4
 
@@ -209,7 +210,12 @@ def tile_gcnfast_t_v_kernel(tc, h, e, AA_mask, GCW, GCB, z, grad_out, out):
                 nc.scalar.copy(
                     out=staged[:, :, m, :], in_=acc[:].rearrange("p (b d) -> p b d", b=GROUP)
                 )
-            nc.sync.dma_start(
-                out=out_rows[:, group * GROUP : (group + 1) * GROUP, :],
-                in_=staged[:].rearrange("p b t d -> p b (t d)"),
-            )
+                pieces = LAST_PIECES if group == GROUPS - 1 else (M_TILES,)
+                if m + 1 in pieces:
+                    first_m = ([0] + list(pieces))[pieces.index(m + 1)]
+                    nc.sync.dma_start(
+                        out=out_rows[
+                            :, group * GROUP : (group + 1) * GROUP, first_m * FEAT : (m + 1) * FEAT
+                        ],
+                        in_=staged[:, :, first_m : m + 1, :].rearrange("p b t d -> p b (t d)"),
+                    )

@@ -31,7 +31,7 @@ PAIR = P // NODES
 PAIRS = BATCH // PAIR
 QUAD = 4
 BANK_BF16 = 1024
-LAST_PIECES = (4, 6, 8)
+LAST_PIECES = (4, 6, 7, 8)
 FIRST_PAIRS = 2
 TURN_BANKS = 4
 
@@ -92,8 +92,14 @@ def tile_gcnfast_t_v_kernel(tc, h, e, AA_mask, GCW, GCB, z, grad_out, out):
             for g in range(PASSES):
                 mask_t = weights.tile([P, PACK, J], BF16)
                 gcw_t = weights.tile([P, PACK, J], BF16)
-                nc.sync.dma_start(out=mask_t[:].rearrange("p u j -> p (u j)"), in_=mask_rows[g])
-                nc.sync.dma_start(out=gcw_t[:].rearrange("p u j -> p (u j)"), in_=gcw_rows[g])
+                if g == 0:
+                    for u in range(PACK):
+                        row = slice(u * J, (u + 1) * J)
+                        nc.sync.dma_start(out=mask_t[:, u, :], in_=mask_rows[g][:, row])
+                        nc.sync.dma_start(out=gcw_t[:, u, :], in_=gcw_rows[g][:, row])
+                else:
+                    nc.sync.dma_start(out=mask_t[:].rearrange("p u j -> p (u j)"), in_=mask_rows[g])
+                    nc.sync.dma_start(out=gcw_t[:].rearrange("p u j -> p (u j)"), in_=gcw_rows[g])
                 mask_tiles.append(mask_t)
                 gcw_tiles.append(gcw_t)
             g_tiles = []
@@ -122,9 +128,13 @@ def tile_gcnfast_t_v_kernel(tc, h, e, AA_mask, GCW, GCB, z, grad_out, out):
                 load_z(pair)
 
             for g in range(PASSES):
-                nc.vector.tensor_tensor(
-                    out=gcw_tiles[g][:], in0=mask_tiles[g][:], in1=gcw_tiles[g][:], op=ALU.mult
-                )
+                for rows in [slice(u, u + 1) for u in range(PACK)] if g == 0 else [slice(0, PACK)]:
+                    nc.vector.tensor_tensor(
+                        out=gcw_tiles[g][:, rows, :],
+                        in0=mask_tiles[g][:, rows, :],
+                        in1=gcw_tiles[g][:, rows, :],
+                        op=ALU.mult,
+                    )
                 nc.vector.tensor_scalar_max(
                     out=a_grouped[:, g, :].rearrange("p (mc th u) -> p mc th u", th=2, u=PACK),
                     in0=gcw_tiles[g][:].rearrange("p u (th mc) -> p mc th u", th=2),
@@ -166,56 +176,93 @@ def tile_gcnfast_t_v_kernel(tc, h, e, AA_mask, GCW, GCB, z, grad_out, out):
                         g_banks.append(turn_back(b))
 
         stores = ctx.enter_context(tc.tile_pool(name="stores", bufs=3))
-        for group in range(GROUPS):
-            dz_grouped = quant.tile([P, PASSES, GROUP, FEAT, PACK], BF16, align_bytes=64)
-            for bl in range(GROUP):
-                b = group * GROUP + bl
-                for g in range(PASSES):
-                    rows = slice(g * PACK, (g + 1) * PACK)
-                    nc.vector.scalar_tensor_tensor(
-                        out=dz_grouped[:, g, bl, :, :],
-                        in0=z_tiles[b // PAIR][:, b % PAIR, rows, :].rearrange("p u d -> p d u"),
-                        scalar=0.0,
-                        in1=g_banks[b][:, g, :, :]
-                        .rearrange("p d u2 -> p (d u2)")
-                        .bitcast(BF16)
-                        .rearrange("p (d u) -> p d u", u=PACK),
-                        op0=ALU.is_gt,
-                        op1=ALU.mult,
-                    )
-                if b + TURN_BANKS < BATCH:
-                    g_banks.append(turn_back(b + TURN_BANKS))
-            dz_codes = quant.tile([P, PASSES, N_TILE], U32, align_bytes=64)
-            dz_scales = quant.tile([P, PASSES, N_TILE], U8, align_bytes=64)
-            nc.vector.quantize_mx(
-                out=dz_codes[:].rearrange("p g n -> p (g n)").bitcast(E5M2_X4),
-                scales=dz_scales[:].rearrange("p g n -> p (g n)"),
-                in_=dz_grouped[:].rearrange("p g b d u -> p (g b d u)"),
+        def mask_rows_of(dz_grouped, b, g):
+            rows = slice(g * PACK, (g + 1) * PACK)
+            nc.vector.scalar_tensor_tensor(
+                out=dz_grouped[:, g, b % GROUP, :, :],
+                in0=z_tiles[b // PAIR][:, b % PAIR, rows, :].rearrange("p u d -> p d u"),
+                scalar=0.0,
+                in1=g_banks[b][:, g, :, :]
+                .rearrange("p d u2 -> p (d u2)")
+                .bitcast(BF16)
+                .rearrange("p (d u) -> p d u", u=PACK),
+                op0=ALU.is_gt,
+                op1=ALU.mult,
             )
 
-            staged = stores.tile([P, GROUP, HALF_STEPS, FEAT], F32)
-            for m in range(M_TILES):
-                cols = slice(m * P, (m + 1) * P)
-                acc = psum.tile([P, N_TILE], F32, tag="acc")
-                for g in range(PASSES):
-                    nc.tensor.matmul_mx(
-                        out=acc[:],
-                        lhsT=a_codes[:, g, cols].bitcast(E4M3_X4),
-                        lhsT_scale=a_scales[:, g, cols],
-                        rhs=dz_codes[:, g, :].bitcast(E5M2_X4),
-                        rhs_scale=dz_scales[:, g, :],
-                        start=(g == 0),
-                        stop=(g == PASSES - 1),
-                    )
+        def multiply(acc, dz_codes, dz_scales, m, g):
+            cols = slice(m * P, (m + 1) * P)
+            nc.tensor.matmul_mx(
+                out=acc[:],
+                lhsT=a_codes[:, g, cols].bitcast(E4M3_X4),
+                lhsT_scale=a_scales[:, g, cols],
+                rhs=dz_codes[:, g, :].bitcast(E5M2_X4),
+                rhs_scale=dz_scales[:, g, :],
+                start=(g == 0),
+                stop=(g == PASSES - 1),
+            )
+
+        def leave(staged, acc, group, m, pieces, engine):
+            if engine == "vector":
+                nc.vector.tensor_copy(
+                    out=staged[:, :, m, :], in_=acc[:].rearrange("p (b d) -> p b d", b=GROUP)
+                )
+            else:
                 nc.scalar.copy(
                     out=staged[:, :, m, :], in_=acc[:].rearrange("p (b d) -> p b d", b=GROUP)
                 )
-                pieces = LAST_PIECES if group == GROUPS - 1 else (M_TILES,)
-                if m + 1 in pieces:
-                    first_m = ([0] + list(pieces))[pieces.index(m + 1)]
-                    nc.sync.dma_start(
-                        out=out_rows[
-                            :, group * GROUP : (group + 1) * GROUP, first_m * FEAT : (m + 1) * FEAT
-                        ],
-                        in_=staged[:, :, first_m : m + 1, :].rearrange("p b t d -> p b (t d)"),
+            if m + 1 in pieces:
+                first_m = ([0] + list(pieces))[pieces.index(m + 1)]
+                nc.sync.dma_start(
+                    out=out_rows[
+                        :, group * GROUP : (group + 1) * GROUP, first_m * FEAT : (m + 1) * FEAT
+                    ],
+                    in_=staged[:, :, first_m : m + 1, :].rearrange("p b t d -> p b (t d)"),
+                )
+
+        for group in range(GROUPS):
+            last = group == GROUPS - 1
+            dz_grouped = quant.tile([P, PASSES, GROUP, FEAT, PACK], BF16, align_bytes=64)
+            dz_codes = quant.tile([P, PASSES, N_TILE], U32, align_bytes=64)
+            dz_scales = quant.tile([P, PASSES, N_TILE], U8, align_bytes=64)
+            staged = stores.tile([P, GROUP, HALF_STEPS, FEAT], F32)
+            if not last:
+                for bl in range(GROUP):
+                    b = group * GROUP + bl
+                    for g in range(PASSES):
+                        mask_rows_of(dz_grouped, b, g)
+                    if b + TURN_BANKS < BATCH:
+                        g_banks.append(turn_back(b + TURN_BANKS))
+                nc.vector.quantize_mx(
+                    out=dz_codes[:].rearrange("p g n -> p (g n)").bitcast(E5M2_X4),
+                    scales=dz_scales[:].rearrange("p g n -> p (g n)"),
+                    in_=dz_grouped[:].rearrange("p g b d u -> p (g b d u)"),
+                )
+                for m in range(M_TILES):
+                    acc = psum.tile([P, N_TILE], F32, tag="acc")
+                    for g in range(PASSES):
+                        multiply(acc, dz_codes, dz_scales, m, g)
+                    leave(staged, acc, group, m, (M_TILES,), "scalar")
+            else:
+                early = []
+                for g in range(PASSES):
+                    for bl in range(GROUP):
+                        mask_rows_of(dz_grouped, group * GROUP + bl, g)
+                    nc.vector.quantize_mx(
+                        out=dz_codes[:, g, :].bitcast(E5M2_X4),
+                        scales=dz_scales[:, g, :],
+                        in_=dz_grouped[:, g, :, :, :].rearrange("p b d u -> p (b d u)"),
                     )
+                    if g == 0:
+                        for m in range(8 - TURN_BANKS):
+                            acc = psum.tile([P, N_TILE], F32, tag="acc")
+                            multiply(acc, dz_codes, dz_scales, m, 0)
+                            early.append(acc)
+                for m in range(M_TILES):
+                    if m < len(early):
+                        acc = early[m]
+                    else:
+                        acc = psum.tile([P, N_TILE], F32, tag="acc")
+                        multiply(acc, dz_codes, dz_scales, m, 0)
+                    multiply(acc, dz_codes, dz_scales, m, 1)
+                    leave(staged, acc, group, m, LAST_PIECES, "vector" if m % 2 == 1 else "scalar")

@@ -32,6 +32,7 @@ PAIRS = BATCH // PAIR
 QUAD = 4
 BANK_BF16 = 1024
 LAST_PIECES = (4, 6, 7, 8)
+SCALAR_COLUMNS = (192, 128)
 FIRST_PAIRS = 2
 TURN_BANKS = 4
 
@@ -127,6 +128,26 @@ def tile_gcnfast_t_v_kernel(tc, h, e, AA_mask, GCW, GCB, z, grad_out, out):
             for pair in range(FIRST_PAIRS, PAIRS):
                 load_z(pair)
 
+            def grouped_view(g):
+                return a_grouped[:, g, :].rearrange("p (mc th u) -> p mc th u", th=2, u=PACK)
+
+            def product_view(g):
+                return gcw_tiles[g][:].rearrange("p u (th mc) -> p mc th u", th=2)
+
+            def relu_on_scalar(g):
+                nc.scalar.activation(
+                    out=grouped_view(g)[:, : SCALAR_COLUMNS[g], :, :],
+                    in_=product_view(g)[:, : SCALAR_COLUMNS[g], :, :],
+                    func=mybir.ActivationFunctionType.Relu,
+                )
+
+            def quantise_a(g):
+                nc.vector.quantize_mx(
+                    out=a_codes[:, g, :].bitcast(E4M3_X4),
+                    scales=a_scales[:, g, :],
+                    in_=a_grouped[:, g, :],
+                )
+
             for g in range(PASSES):
                 for rows in [slice(u, u + 1) for u in range(PACK)] if g == 0 else [slice(0, PACK)]:
                     nc.vector.tensor_tensor(
@@ -135,17 +156,14 @@ def tile_gcnfast_t_v_kernel(tc, h, e, AA_mask, GCW, GCB, z, grad_out, out):
                         in1=gcw_tiles[g][:, rows, :],
                         op=ALU.mult,
                     )
+                if g == 0:
+                    relu_on_scalar(g)
                 nc.vector.tensor_scalar_max(
-                    out=a_grouped[:, g, :].rearrange("p (mc th u) -> p mc th u", th=2, u=PACK),
-                    in0=gcw_tiles[g][:].rearrange("p u (th mc) -> p mc th u", th=2),
+                    out=grouped_view(g)[:, SCALAR_COLUMNS[g] :, :, :],
+                    in0=product_view(g)[:, SCALAR_COLUMNS[g] :, :, :],
                     scalar1=0.0,
                 )
-            for g in range(PASSES):
-                nc.vector.quantize_mx(
-                    out=a_codes[:, g, :].bitcast(E4M3_X4),
-                    scales=a_scales[:, g, :],
-                    in_=a_grouped[:, g, :],
-                )
+            quantise_a(0)
 
             for pair in range(PAIRS):
                 batches = slice(pair * PAIR, (pair + 1) * PAIR)
@@ -174,6 +192,8 @@ def tile_gcnfast_t_v_kernel(tc, h, e, AA_mask, GCW, GCB, z, grad_out, out):
                 if pair == FIRST_PAIRS - 1:
                     for b in range(TURN_BANKS):
                         g_banks.append(turn_back(b))
+                    relu_on_scalar(1)
+                    quantise_a(1)
 
         stores = ctx.enter_context(tc.tile_pool(name="stores", bufs=3))
         def mask_rows_of(dz_grouped, b, g):
@@ -233,11 +253,12 @@ def tile_gcnfast_t_v_kernel(tc, h, e, AA_mask, GCW, GCB, z, grad_out, out):
                         mask_rows_of(dz_grouped, b, g)
                     if b + TURN_BANKS < BATCH:
                         g_banks.append(turn_back(b + TURN_BANKS))
-                nc.vector.quantize_mx(
-                    out=dz_codes[:].rearrange("p g n -> p (g n)").bitcast(E5M2_X4),
-                    scales=dz_scales[:].rearrange("p g n -> p (g n)"),
-                    in_=dz_grouped[:].rearrange("p g b d u -> p (g b d u)"),
-                )
+                for g in range(PASSES):
+                    nc.vector.quantize_mx(
+                        out=dz_codes[:, g, :].bitcast(E5M2_X4),
+                        scales=dz_scales[:, g, :],
+                        in_=dz_grouped[:, g, :, :, :].rearrange("p b d u -> p (b d u)"),
+                    )
                 for m in range(M_TILES):
                     acc = psum.tile([P, N_TILE], F32, tag="acc")
                     for g in range(PASSES):
@@ -245,24 +266,28 @@ def tile_gcnfast_t_v_kernel(tc, h, e, AA_mask, GCW, GCB, z, grad_out, out):
                     leave(staged, acc, group, m, (M_TILES,), "scalar")
             else:
                 early = []
+                late = []
                 for g in range(PASSES):
                     for bl in range(GROUP):
                         mask_rows_of(dz_grouped, group * GROUP + bl, g)
-                    nc.vector.quantize_mx(
-                        out=dz_codes[:, g, :].bitcast(E5M2_X4),
-                        scales=dz_scales[:, g, :],
-                        in_=dz_grouped[:, g, :, :, :].rearrange("p b d u -> p (b d u)"),
-                    )
+                        if g == PASSES - 1:
+                            acc = turn_psum.tile([P, N_TILE], F32, tag="turn")
+                            multiply(acc, dz_codes, dz_scales, len(early) + bl, 0)
+                            late.append(acc)
+                    for half in range(2):
+                        batches = slice(half * PAIR, (half + 1) * PAIR)
+                        columns = slice(half * PAIR * FEAT, (half + 1) * PAIR * FEAT)
+                        nc.vector.quantize_mx(
+                            out=dz_codes[:, g, columns].bitcast(E5M2_X4),
+                            scales=dz_scales[:, g, columns],
+                            in_=dz_grouped[:, g, batches, :, :].rearrange("p b d u -> p (b d u)"),
+                        )
                     if g == 0:
                         for m in range(8 - TURN_BANKS):
                             acc = psum.tile([P, N_TILE], F32, tag="acc")
                             multiply(acc, dz_codes, dz_scales, m, 0)
                             early.append(acc)
                 for m in range(M_TILES):
-                    if m < len(early):
-                        acc = early[m]
-                    else:
-                        acc = psum.tile([P, N_TILE], F32, tag="acc")
-                        multiply(acc, dz_codes, dz_scales, m, 0)
+                    acc = (early + late)[m]
                     multiply(acc, dz_codes, dz_scales, m, 1)
                     leave(staged, acc, group, m, LAST_PIECES, "vector" if m % 2 == 1 else "scalar")

@@ -35,6 +35,10 @@ LAST_PIECES = (4, 6, 7, 8)
 SCALAR_COLUMNS = (192, 128)
 FIRST_PAIRS = 2
 TURN_BANKS = 4
+LAST_PAIRS = range(PAIRS - GROUP // PAIR, PAIRS)
+TURN_ORDER = [(pair, g) for pair in range(PAIRS - GROUP // PAIR) for g in range(PASSES)] + [
+    (pair, g) for g in range(PASSES) for pair in LAST_PAIRS
+]
 
 FLOPS = 2 * I * J * BATCH * FEAT
 BYTES = 2 * (2 * I * J) + 4 * BATCH * I * FEAT + 2 * BATCH * I * FEAT + 4 * BATCH * J * FEAT
@@ -63,26 +67,26 @@ def tile_gcnfast_t_v_kernel(tc, h, e, AA_mask, GCW, GCB, z, grad_out, out):
         masks.make_identity(nc, ident_words[:])
         sorter = keep.tile([P, P], BF16)
         nc.vector.tensor_copy(
-            out=sorter[:].bitcast(F32).rearrange("i (bl u2 s4) -> i bl u2 s4", bl=PAIR, u2=2),
-            in_=ident[:].bitcast(F32).rearrange("i (bl s4 u2) -> i bl u2 s4", bl=PAIR, u2=2),
+            out=sorter[:].rearrange("i (u s4 bl) -> i u s4 bl", u=PACK, bl=PAIR),
+            in_=ident[:].rearrange("i (bl s4 u) -> i u s4 bl", u=PACK, bl=PAIR),
         )
         a_grouped = keep.tile([P, PASSES, J * PACK], BF16, align_bytes=64)
         a_codes = keep.tile([P, PASSES, J], U32, align_bytes=64)
         a_scales = keep.tile([P, PASSES, J], U8, align_bytes=64)
-        by_feature = keep.tile([P, PASSES, BATCH, 2, P, 2], BF16)
+        by_feature = keep.tile([P, PASSES, PAIRS, PACK, P, PAIR], BF16)
 
-        def turn_back(b):
-            bank_back = turn_psum.tile([P, PASSES, FEAT, 2], F32, tag="turn")
-            for g in range(PASSES):
-                for u2 in range(2):
-                    nc.tensor.transpose(
-                        out=bank_back[:, g, :, u2],
-                        in_=by_feature[:, g, b, u2, :, :].rearrange("d p e -> d (p e)").bitcast(F32),
-                        identity=ident_words[:],
-                    )
-            return bank_back
+        g_banks = {}
 
-        g_banks = []
+        def turn_back():
+            pair, g = TURN_ORDER[len(g_banks)]
+            bank_back = turn_psum.tile([P, PACK, FEAT], F32, tag="turn")
+            for u in range(PACK):
+                nc.tensor.transpose(
+                    out=bank_back[:, u, :],
+                    in_=by_feature[:, g, pair, u, :, :].rearrange("d p bl -> d (p bl)").bitcast(F32),
+                    identity=ident_words[:],
+                )
+            g_banks[(pair, g)] = bank_back
 
         with ExitStack() as head:
             weights = head.enter_context(tc.tile_pool(name="weights", bufs=PASSES))
@@ -166,7 +170,6 @@ def tile_gcnfast_t_v_kernel(tc, h, e, AA_mask, GCW, GCB, z, grad_out, out):
             quantise_a(0)
 
             for pair in range(PAIRS):
-                batches = slice(pair * PAIR, (pair + 1) * PAIR)
                 for quad in range(STEPS // QUAD):
                     bank_in = psum.tile([P, BANK_BF16], BF16, tag="acc")
                     for k in range(QUAD):
@@ -178,37 +181,43 @@ def tile_gcnfast_t_v_kernel(tc, h, e, AA_mask, GCW, GCB, z, grad_out, out):
                     g = quad * QUAD // HALF_STEPS
                     first_p = (quad * QUAD % HALF_STEPS) * QUARTETS
                     nc.scalar.copy(
-                        out=by_feature[:, g, batches, :, :, :]
-                        .rearrange("d bl u2 p e -> d (bl u2 p e)")
+                        out=by_feature[:, g, pair, :, :, :]
+                        .rearrange("d u p bl -> d (u p bl)")
                         .bitcast(F32)
-                        .rearrange("d (blu p) -> d blu p", p=P)[
+                        .rearrange("d (u p) -> d u p", p=P)[
                             :, :, first_p : first_p + QUAD * QUARTETS
                         ]
-                        .rearrange("d blu (k s4) -> d blu k s4", k=QUAD),
+                        .rearrange("d u (k s4) -> d u k s4", k=QUAD),
                         in_=bank_in[:, : QUAD * P]
                         .bitcast(F32)
-                        .rearrange("d (k blu s4) -> d blu k s4", k=QUAD, s4=QUARTETS),
+                        .rearrange("d (k u s4) -> d u k s4", k=QUAD, s4=QUARTETS),
                     )
                 if pair == FIRST_PAIRS - 1:
-                    for b in range(TURN_BANKS):
-                        g_banks.append(turn_back(b))
+                    for turn in range(TURN_BANKS):
+                        turn_back()
                     relu_on_scalar(1)
                     quantise_a(1)
 
         stores = ctx.enter_context(tc.tile_pool(name="stores", bufs=3))
-        def mask_rows_of(dz_grouped, b, g):
+        def mask_pair(dz_grouped, pair, g):
             rows = slice(g * PACK, (g + 1) * PACK)
-            nc.vector.scalar_tensor_tensor(
-                out=dz_grouped[:, g, b % GROUP, :, :],
-                in0=z_tiles[b // PAIR][:, b % PAIR, rows, :].rearrange("p u d -> p d u"),
-                scalar=0.0,
-                in1=g_banks[b][:, g, :, :]
-                .rearrange("p d u2 -> p (d u2)")
+            turned = (
+                g_banks[(pair, g)][:]
+                .rearrange("p u d -> p (u d)")
                 .bitcast(BF16)
-                .rearrange("p (d u) -> p d u", u=PACK),
-                op0=ALU.is_gt,
-                op1=ALU.mult,
+                .rearrange("p (u d bl) -> p bl d u", u=PACK, bl=PAIR)
             )
+            for bl in range(PAIR):
+                nc.vector.scalar_tensor_tensor(
+                    out=dz_grouped[:, g, (pair * PAIR + bl) % GROUP, :, :],
+                    in0=z_tiles[pair][:, bl, rows, :].rearrange("p u d -> p d u"),
+                    scalar=0.0,
+                    in1=turned[:, bl, :, :],
+                    op0=ALU.is_gt,
+                    op1=ALU.mult,
+                )
+            if len(g_banks) < len(TURN_ORDER):
+                turn_back()
 
         def multiply(acc, dz_codes, dz_scales, m, g):
             cols = slice(m * P, (m + 1) * P)
@@ -247,12 +256,9 @@ def tile_gcnfast_t_v_kernel(tc, h, e, AA_mask, GCW, GCB, z, grad_out, out):
             dz_scales = quant.tile([P, PASSES, N_TILE], U8, align_bytes=64)
             staged = stores.tile([P, GROUP, HALF_STEPS, FEAT], F32)
             if not last:
-                for bl in range(GROUP):
-                    b = group * GROUP + bl
+                for pair in range(group * GROUP // PAIR, (group + 1) * GROUP // PAIR):
                     for g in range(PASSES):
-                        mask_rows_of(dz_grouped, b, g)
-                    if b + TURN_BANKS < BATCH:
-                        g_banks.append(turn_back(b + TURN_BANKS))
+                        mask_pair(dz_grouped, pair, g)
                 for g in range(PASSES):
                     nc.vector.quantize_mx(
                         out=dz_codes[:, g, :].bitcast(E5M2_X4),
@@ -267,13 +273,17 @@ def tile_gcnfast_t_v_kernel(tc, h, e, AA_mask, GCW, GCB, z, grad_out, out):
             else:
                 early = []
                 late = []
+
+                def open_late():
+                    acc = turn_psum.tile([P, N_TILE], F32, tag="turn")
+                    multiply(acc, dz_codes, dz_scales, len(early) + len(late), 0)
+                    late.append(acc)
+
                 for g in range(PASSES):
-                    for bl in range(GROUP):
-                        mask_rows_of(dz_grouped, group * GROUP + bl, g)
+                    for pair in range(PAIRS - GROUP // PAIR, PAIRS):
+                        mask_pair(dz_grouped, pair, g)
                         if g == PASSES - 1:
-                            acc = turn_psum.tile([P, N_TILE], F32, tag="turn")
-                            multiply(acc, dz_codes, dz_scales, len(early) + bl, 0)
-                            late.append(acc)
+                            open_late()
                     for half in range(2):
                         batches = slice(half * PAIR, (half + 1) * PAIR)
                         columns = slice(half * PAIR * FEAT, (half + 1) * PAIR * FEAT)
@@ -287,6 +297,8 @@ def tile_gcnfast_t_v_kernel(tc, h, e, AA_mask, GCW, GCB, z, grad_out, out):
                             acc = psum.tile([P, N_TILE], F32, tag="acc")
                             multiply(acc, dz_codes, dz_scales, m, 0)
                             early.append(acc)
+                        for pair in range(GROUP // PAIR):
+                            open_late()
                 for m in range(M_TILES):
                     acc = (early + late)[m]
                     multiply(acc, dz_codes, dz_scales, m, 1)

@@ -31,6 +31,7 @@ PAIR = P // NODES
 PAIRS = BATCH // PAIR
 QUAD = 4
 BANK_BF16 = 1024
+HALVES = (4, 8)
 LAST_PIECES = (4, 6, 7, 8)
 SCALAR_COLUMNS = (192, 128)
 FIRST_PAIRS = 2
@@ -50,12 +51,13 @@ def tile_gcnfast_t_v_kernel(tc, h, e, AA_mask, GCW, GCB, z, grad_out, out):
     mask_rows = AA_mask.rearrange("(g p u) j -> g p (u j)", p=P, u=PACK)
     gcw_rows = GCW.rearrange("(g p u) j -> g p (u j)", p=P, u=PACK)
     z_rows = z.rearrange("b (g p u) d -> p (b g) (u d)", p=P, u=PACK)
+    z_passes = z.rearrange("b (g p u) d -> g p b (u d)", p=P, u=PACK)
     g_pairs = grad_out.rearrange("(pair bl) s t d -> pair (bl s) t d", bl=PAIR)
     out_rows = out.rearrange("b c t d -> b (c t d)").rearrange("b (q r) -> q b r", q=P)
 
     with ExitStack() as ctx:
         keep = ctx.enter_context(tc.tile_pool(name="keep", bufs=1))
-        loads = ctx.enter_context(tc.tile_pool(name="loads", bufs=6))
+        loads = ctx.enter_context(tc.tile_pool(name="loads", bufs=PAIRS))
         quant = ctx.enter_context(tc.tile_pool(name="quant", bufs=2))
         turn_psum = ctx.enter_context(tc.psum_pool(name="turn_psum", bufs=TURN_BANKS))
         psum = ctx.enter_context(tc.psum_pool(name="psum", bufs=8 - TURN_BANKS))
@@ -88,6 +90,34 @@ def tile_gcnfast_t_v_kernel(tc, h, e, AA_mask, GCW, GCB, z, grad_out, out):
                 )
             g_banks[(pair, g)] = bank_back
 
+        z_tiles = []
+        last_z = []
+
+        def new_dz():
+            return quant.tile([P, PASSES, GROUP, FEAT, PACK], BF16, align_bytes=64, name="dz_grouped")
+
+        def mask_pair(dz_grouped, pair, g):
+            rows = slice(g * PACK, (g + 1) * PACK)
+            turned = (
+                g_banks[(pair, g)][:]
+                .rearrange("p u d -> p (u d)")
+                .bitcast(BF16)
+                .rearrange("p (u d bl) -> p bl d u", u=PACK, bl=PAIR)
+            )
+            for bl in range(PAIR):
+                place = (pair * PAIR + bl) % GROUP
+                z_block = last_z[g][:, place, :, :] if pair in LAST_PAIRS else z_tiles[pair][:, bl, rows, :]
+                nc.vector.scalar_tensor_tensor(
+                    out=dz_grouped[:, g, place, :, :],
+                    in0=z_block.rearrange("p u d -> p d u"),
+                    scalar=0.0,
+                    in1=turned[:, bl, :, :],
+                    op0=ALU.is_gt,
+                    op1=ALU.mult,
+                )
+            if len(g_banks) < len(TURN_ORDER):
+                turn_back()
+
         with ExitStack() as head:
             weights = head.enter_context(tc.tile_pool(name="weights", bufs=PASSES))
             as_it_lies = head.enter_context(tc.tile_pool(name="as_it_lies", bufs=PAIRS))
@@ -108,7 +138,6 @@ def tile_gcnfast_t_v_kernel(tc, h, e, AA_mask, GCW, GCB, z, grad_out, out):
                 mask_tiles.append(mask_t)
                 gcw_tiles.append(gcw_t)
             g_tiles = []
-            z_tiles = []
 
             def load_g(pair):
                 g_t = as_it_lies.tile([P, STEPS, FEAT], BF16)
@@ -116,21 +145,33 @@ def tile_gcnfast_t_v_kernel(tc, h, e, AA_mask, GCW, GCB, z, grad_out, out):
                 g_tiles.append(g_t)
 
             def load_z(pair):
-                z_t = loads.tile([P, PAIR, ROWS, FEAT], F32)
-                nc.sync.dma_start(
-                    out=z_t[:].rearrange("p b (g u) d -> p (b g) (u d)", u=PACK),
-                    in_=z_rows[:, pair * PAIR * PASSES : (pair + 1) * PAIR * PASSES, :],
-                )
+                z_t = loads.tile([P, PAIR, ROWS, FEAT], F32, tag="z")
+                if pair == FIRST_PAIRS:
+                    for g in range(PASSES):
+                        nc.sync.dma_start(
+                            out=z_t[:, :, g * PACK : (g + 1) * PACK, :].rearrange("p b u d -> p b (u d)"),
+                            in_=z_passes[g][:, pair * PAIR : (pair + 1) * PAIR, :],
+                        )
+                else:
+                    nc.sync.dma_start(
+                        out=z_t[:].rearrange("p b (g u) d -> p (b g) (u d)", u=PACK),
+                        in_=z_rows[:, pair * PAIR * PASSES : (pair + 1) * PAIR * PASSES, :],
+                    )
                 z_tiles.append(z_t)
 
-            for pair in range(FIRST_PAIRS):
+            for pair in range(PAIRS - GROUP // PAIR):
                 load_g(pair)
             for pair in range(FIRST_PAIRS):
                 load_z(pair)
-            for pair in range(FIRST_PAIRS, PAIRS):
-                load_g(pair)
-            for pair in range(FIRST_PAIRS, PAIRS):
+                load_g(LAST_PAIRS[pair])
+            for pair in range(FIRST_PAIRS, PAIRS - GROUP // PAIR):
                 load_z(pair)
+            for g in range(PASSES):
+                z_t = loads.tile([P, GROUP, PACK, FEAT], F32, tag="z")
+                nc.sync.dma_start(
+                    out=z_t[:].rearrange("p b u d -> p b (u d)"), in_=z_passes[g][:, BATCH - GROUP :, :]
+                )
+                last_z.append(z_t)
 
             def grouped_view(g):
                 return a_grouped[:, g, :].rearrange("p (mc th u) -> p mc th u", th=2, u=PACK)
@@ -169,7 +210,7 @@ def tile_gcnfast_t_v_kernel(tc, h, e, AA_mask, GCW, GCB, z, grad_out, out):
                 )
             quantise_a(0)
 
-            for pair in range(PAIRS):
+            def first_turn(pair):
                 for quad in range(STEPS // QUAD):
                     bank_in = psum.tile([P, BANK_BF16], BF16, tag="acc")
                     for k in range(QUAD):
@@ -192,33 +233,24 @@ def tile_gcnfast_t_v_kernel(tc, h, e, AA_mask, GCW, GCB, z, grad_out, out):
                         .bitcast(F32)
                         .rearrange("d (k u s4) -> d u k s4", k=QUAD, s4=QUARTETS),
                     )
-                if pair == FIRST_PAIRS - 1:
-                    for turn in range(TURN_BANKS):
-                        turn_back()
-                    relu_on_scalar(1)
-                    quantise_a(1)
+
+            for pair in range(FIRST_PAIRS):
+                first_turn(pair)
+            for turn in range(TURN_BANKS):
+                turn_back()
+            relu_on_scalar(1)
+            quantise_a(1)
+            for pair in range(FIRST_PAIRS, PAIRS - GROUP // PAIR):
+                first_turn(pair)
+            dz_grouped = new_dz()
+            mask_pair(dz_grouped, 0, 0)
+            first_turn(LAST_PAIRS[0])
+            mask_pair(dz_grouped, 0, 1)
+            mask_pair(dz_grouped, 1, 0)
+            first_turn(LAST_PAIRS[1])
+            mask_pair(dz_grouped, 1, 1)
 
         stores = ctx.enter_context(tc.tile_pool(name="stores", bufs=3))
-        def mask_pair(dz_grouped, pair, g):
-            rows = slice(g * PACK, (g + 1) * PACK)
-            turned = (
-                g_banks[(pair, g)][:]
-                .rearrange("p u d -> p (u d)")
-                .bitcast(BF16)
-                .rearrange("p (u d bl) -> p bl d u", u=PACK, bl=PAIR)
-            )
-            for bl in range(PAIR):
-                nc.vector.scalar_tensor_tensor(
-                    out=dz_grouped[:, g, (pair * PAIR + bl) % GROUP, :, :],
-                    in0=z_tiles[pair][:, bl, rows, :].rearrange("p u d -> p d u"),
-                    scalar=0.0,
-                    in1=turned[:, bl, :, :],
-                    op0=ALU.is_gt,
-                    op1=ALU.mult,
-                )
-            if len(g_banks) < len(TURN_ORDER):
-                turn_back()
-
         def multiply(acc, dz_codes, dz_scales, m, g):
             cols = slice(m * P, (m + 1) * P)
             nc.tensor.matmul_mx(
@@ -251,14 +283,16 @@ def tile_gcnfast_t_v_kernel(tc, h, e, AA_mask, GCW, GCB, z, grad_out, out):
 
         for group in range(GROUPS):
             last = group == GROUPS - 1
-            dz_grouped = quant.tile([P, PASSES, GROUP, FEAT, PACK], BF16, align_bytes=64)
+            if group > 0:
+                dz_grouped = new_dz()
             dz_codes = quant.tile([P, PASSES, N_TILE], U32, align_bytes=64)
             dz_scales = quant.tile([P, PASSES, N_TILE], U8, align_bytes=64)
             staged = stores.tile([P, GROUP, HALF_STEPS, FEAT], F32)
             if not last:
-                for pair in range(group * GROUP // PAIR, (group + 1) * GROUP // PAIR):
-                    for g in range(PASSES):
-                        mask_pair(dz_grouped, pair, g)
+                if group > 0:
+                    for pair in range(group * GROUP // PAIR, (group + 1) * GROUP // PAIR):
+                        for g in range(PASSES):
+                            mask_pair(dz_grouped, pair, g)
                 for g in range(PASSES):
                     nc.vector.quantize_mx(
                         out=dz_codes[:, g, :].bitcast(E5M2_X4),
@@ -269,7 +303,7 @@ def tile_gcnfast_t_v_kernel(tc, h, e, AA_mask, GCW, GCB, z, grad_out, out):
                     acc = psum.tile([P, N_TILE], F32, tag="acc")
                     for g in range(PASSES):
                         multiply(acc, dz_codes, dz_scales, m, g)
-                    leave(staged, acc, group, m, (M_TILES,), "scalar")
+                    leave(staged, acc, group, m, HALVES if group == GROUPS - 2 else (M_TILES,), "scalar")
             else:
                 early = []
                 late = []

@@ -32,7 +32,7 @@ PAIRS = BATCH // PAIR
 QUAD = 4
 BANK_BF16 = 1024
 HALVES = (4, 8)
-LAST_PIECES = (4, 6, 7, 8)
+FIRST_ROWS = (slice(0, 1), slice(1, 2), slice(2, 4))
 SCALAR_COLUMNS = (192, 128)
 FIRST_PAIRS = 2
 TURN_BANKS = 4
@@ -52,12 +52,12 @@ def tile_gcnfast_t_v_kernel(tc, h, e, AA_mask, GCW, GCB, z, grad_out, out):
     gcw_rows = GCW.rearrange("(g p u) j -> g p (u j)", p=P, u=PACK)
     z_rows = z.rearrange("b (g p u) d -> p (b g) (u d)", p=P, u=PACK)
     z_passes = z.rearrange("b (g p u) d -> g p b (u d)", p=P, u=PACK)
-    g_pairs = grad_out.rearrange("(pair bl) s t d -> pair (bl s) t d", bl=PAIR)
+    g_pairs = grad_out.rearrange("(pair bl) s t d -> (bl s) pair (t d)", bl=PAIR)
     out_rows = out.rearrange("b c t d -> b (c t d)").rearrange("b (q r) -> q b r", q=P)
 
     with ExitStack() as ctx:
         keep = ctx.enter_context(tc.tile_pool(name="keep", bufs=1))
-        loads = ctx.enter_context(tc.tile_pool(name="loads", bufs=PAIRS))
+        loads = ctx.enter_context(tc.tile_pool(name="loads", bufs=1))
         quant = ctx.enter_context(tc.tile_pool(name="quant", bufs=2))
         turn_psum = ctx.enter_context(tc.psum_pool(name="turn_psum", bufs=TURN_BANKS))
         psum = ctx.enter_context(tc.psum_pool(name="psum", bufs=8 - TURN_BANKS))
@@ -120,7 +120,7 @@ def tile_gcnfast_t_v_kernel(tc, h, e, AA_mask, GCW, GCB, z, grad_out, out):
 
         with ExitStack() as head:
             weights = head.enter_context(tc.tile_pool(name="weights", bufs=PASSES))
-            as_it_lies = head.enter_context(tc.tile_pool(name="as_it_lies", bufs=PAIRS))
+            as_it_lies = head.enter_context(tc.tile_pool(name="as_it_lies", bufs=1))
 
             mask_tiles = []
             gcw_tiles = []
@@ -128,10 +128,14 @@ def tile_gcnfast_t_v_kernel(tc, h, e, AA_mask, GCW, GCB, z, grad_out, out):
                 mask_t = weights.tile([P, PACK, J], BF16)
                 gcw_t = weights.tile([P, PACK, J], BF16)
                 if g == 0:
-                    for u in range(PACK):
-                        row = slice(u * J, (u + 1) * J)
-                        nc.sync.dma_start(out=mask_t[:, u, :], in_=mask_rows[g][:, row])
-                        nc.sync.dma_start(out=gcw_t[:, u, :], in_=gcw_rows[g][:, row])
+                    for rows in FIRST_ROWS:
+                        run = slice(rows.start * J, rows.stop * J)
+                        nc.sync.dma_start(
+                            out=mask_t[:, rows, :].rearrange("p u j -> p (u j)"), in_=mask_rows[g][:, run]
+                        )
+                        nc.sync.dma_start(
+                            out=gcw_t[:, rows, :].rearrange("p u j -> p (u j)"), in_=gcw_rows[g][:, run]
+                        )
                 else:
                     nc.sync.dma_start(out=mask_t[:].rearrange("p u j -> p (u j)"), in_=mask_rows[g])
                     nc.sync.dma_start(out=gcw_t[:].rearrange("p u j -> p (u j)"), in_=gcw_rows[g])
@@ -139,35 +143,33 @@ def tile_gcnfast_t_v_kernel(tc, h, e, AA_mask, GCW, GCB, z, grad_out, out):
                 gcw_tiles.append(gcw_t)
             g_tiles = []
 
-            def load_g(pair):
-                g_t = as_it_lies.tile([P, STEPS, FEAT], BF16)
-                nc.sync.dma_start(out=g_t[:], in_=g_pairs[pair])
-                g_tiles.append(g_t)
+            def load_g(pair, pairs):
+                g_t = as_it_lies.tile([P, pairs, STEPS, FEAT], BF16, name="grad_%d" % pair)
+                nc.sync.dma_start(
+                    out=g_t[:].rearrange("p q t d -> p q (t d)"), in_=g_pairs[:, pair : pair + pairs, :]
+                )
+                for q in range(pairs):
+                    g_tiles.append(g_t[:, q, :, :])
 
-            def load_z(pair):
-                z_t = loads.tile([P, PAIR, ROWS, FEAT], F32, tag="z")
-                if pair == FIRST_PAIRS:
-                    for g in range(PASSES):
-                        nc.sync.dma_start(
-                            out=z_t[:, :, g * PACK : (g + 1) * PACK, :].rearrange("p b u d -> p b (u d)"),
-                            in_=z_passes[g][:, pair * PAIR : (pair + 1) * PAIR, :],
-                        )
-                else:
-                    nc.sync.dma_start(
-                        out=z_t[:].rearrange("p b (g u) d -> p (b g) (u d)", u=PACK),
-                        in_=z_rows[:, pair * PAIR * PASSES : (pair + 1) * PAIR * PASSES, :],
-                    )
-                z_tiles.append(z_t)
+            def load_z(pair, pairs):
+                z_t = loads.tile([P, pairs * PAIR, ROWS, FEAT], F32, name="z_%d" % pair)
+                nc.sync.dma_start(
+                    out=z_t[:].rearrange("p b (g u) d -> p (b g) (u d)", u=PACK),
+                    in_=z_rows[:, pair * PAIR * PASSES : (pair + pairs) * PAIR * PASSES, :],
+                )
+                for q in range(pairs):
+                    z_tiles.append(z_t[:, q * PAIR : (q + 1) * PAIR, :, :])
 
-            for pair in range(PAIRS - GROUP // PAIR):
-                load_g(pair)
+            for pair in range(0, PAIRS - GROUP // PAIR, 2):
+                load_g(pair, 2)
             for pair in range(FIRST_PAIRS):
-                load_z(pair)
-                load_g(LAST_PAIRS[pair])
-            for pair in range(FIRST_PAIRS, PAIRS - GROUP // PAIR):
-                load_z(pair)
+                load_z(pair, 1)
+                load_g(LAST_PAIRS[pair], 1)
+            for pair in range(FIRST_PAIRS, 2 * FIRST_PAIRS):
+                load_z(pair, 1)
+            load_z(2 * FIRST_PAIRS, 2)
             for g in range(PASSES):
-                z_t = loads.tile([P, GROUP, PACK, FEAT], F32, tag="z")
+                z_t = loads.tile([P, GROUP, PACK, FEAT], F32, name="last_z_%d" % g)
                 nc.sync.dma_start(
                     out=z_t[:].rearrange("p b u d -> p b (u d)"), in_=z_passes[g][:, BATCH - GROUP :, :]
                 )
@@ -194,7 +196,7 @@ def tile_gcnfast_t_v_kernel(tc, h, e, AA_mask, GCW, GCB, z, grad_out, out):
                 )
 
             for g in range(PASSES):
-                for rows in [slice(u, u + 1) for u in range(PACK)] if g == 0 else [slice(0, PACK)]:
+                for rows in FIRST_ROWS if g == 0 else [slice(0, PACK)]:
                     nc.vector.tensor_tensor(
                         out=gcw_tiles[g][:, rows, :],
                         in0=mask_tiles[g][:, rows, :],
@@ -336,4 +338,4 @@ def tile_gcnfast_t_v_kernel(tc, h, e, AA_mask, GCW, GCB, z, grad_out, out):
                 for m in range(M_TILES):
                     acc = (early + late)[m]
                     multiply(acc, dz_codes, dz_scales, m, 1)
-                    leave(staged, acc, group, m, LAST_PIECES, "vector" if m % 2 == 1 else "scalar")
+                    leave(staged, acc, group, m, HALVES, "vector" if m % 2 == 1 else "scalar")

@@ -32,8 +32,8 @@ PAIRS = BATCH // PAIR
 QUAD = 4
 BANK_BF16 = 1024
 HALVES = (4, 8)
-FIRST_ROWS = (slice(0, 1), slice(1, 2), slice(2, 4))
-SCALAR_COLUMNS = (192, 128)
+ROW_HALVES = (slice(0, 2), slice(2, 4))
+SCALAR_COLUMNS = (288, 128)
 FIRST_PAIRS = 2
 TURN_BANKS = 4
 LAST_PAIRS = range(PAIRS - GROUP // PAIR, PAIRS)
@@ -72,6 +72,8 @@ def tile_gcnfast_t_v_kernel(tc, h, e, AA_mask, GCW, GCB, z, grad_out, out):
             out=sorter[:].rearrange("i (u s4 bl) -> i u s4 bl", u=PACK, bl=PAIR),
             in_=ident[:].rearrange("i (bl s4 u) -> i u s4 bl", u=PACK, bl=PAIR),
         )
+        warm = keep.tile([P, 1], F32)
+        nc.scalar.activation(out=warm[:], in_=ident_words[:, 0:1], func=mybir.ActivationFunctionType.Relu)
         a_grouped = keep.tile([P, PASSES, J * PACK], BF16, align_bytes=64)
         a_codes = keep.tile([P, PASSES, J], U32, align_bytes=64)
         a_scales = keep.tile([P, PASSES, J], U8, align_bytes=64)
@@ -127,24 +129,21 @@ def tile_gcnfast_t_v_kernel(tc, h, e, AA_mask, GCW, GCB, z, grad_out, out):
             for g in range(PASSES):
                 mask_t = weights.tile([P, PACK, J], BF16)
                 gcw_t = weights.tile([P, PACK, J], BF16)
-                if g == 0:
-                    for rows in FIRST_ROWS:
-                        run = slice(rows.start * J, rows.stop * J)
-                        nc.sync.dma_start(
-                            out=mask_t[:, rows, :].rearrange("p u j -> p (u j)"), in_=mask_rows[g][:, run]
-                        )
-                        nc.sync.dma_start(
-                            out=gcw_t[:, rows, :].rearrange("p u j -> p (u j)"), in_=gcw_rows[g][:, run]
-                        )
-                else:
-                    nc.sync.dma_start(out=mask_t[:].rearrange("p u j -> p (u j)"), in_=mask_rows[g])
-                    nc.sync.dma_start(out=gcw_t[:].rearrange("p u j -> p (u j)"), in_=gcw_rows[g])
+                for rows in ROW_HALVES:
+                    run = slice(rows.start * J, rows.stop * J)
+                    nc.sync.dma_start(
+                        out=mask_t[:, rows, :].rearrange("p u j -> p (u j)"), in_=mask_rows[g][:, run]
+                    )
+                    nc.sync.dma_start(
+                        out=gcw_t[:, rows, :].rearrange("p u j -> p (u j)"), in_=gcw_rows[g][:, run]
+                    )
                 mask_tiles.append(mask_t)
                 gcw_tiles.append(gcw_t)
             g_tiles = []
 
             def load_g(pair, pairs):
-                g_t = as_it_lies.tile([P, pairs, STEPS, FEAT], BF16, name="grad_%d" % pair)
+                pool = loads if pair == LAST_PAIRS[1] else as_it_lies
+                g_t = pool.tile([P, pairs, STEPS, FEAT], BF16, name="grad_%d" % pair)
                 nc.sync.dma_start(
                     out=g_t[:].rearrange("p q t d -> p q (t d)"), in_=g_pairs[:, pair : pair + pairs, :]
                 )
@@ -160,14 +159,17 @@ def tile_gcnfast_t_v_kernel(tc, h, e, AA_mask, GCW, GCB, z, grad_out, out):
                 for q in range(pairs):
                     z_tiles.append(z_t[:, q * PAIR : (q + 1) * PAIR, :, :])
 
-            for pair in range(0, PAIRS - GROUP // PAIR, 2):
+            for pair in range(0, 2 * FIRST_PAIRS, 2):
                 load_g(pair, 2)
-            for pair in range(FIRST_PAIRS):
-                load_z(pair, 1)
-                load_g(LAST_PAIRS[pair], 1)
-            for pair in range(FIRST_PAIRS, 2 * FIRST_PAIRS):
-                load_z(pair, 1)
-            load_z(2 * FIRST_PAIRS, 2)
+            load_z(0, 1)
+            load_g(2 * FIRST_PAIRS, 2)
+            load_z(1, 1)
+            load_g(LAST_PAIRS[0], 1)
+            load_z(2, 1)
+            load_g(LAST_PAIRS[1], 1)
+            load_z(3, 1)
+            load_z(4, 1)
+            load_z(5, 1)
             for g in range(PASSES):
                 z_t = loads.tile([P, GROUP, PACK, FEAT], F32, name="last_z_%d" % g)
                 nc.sync.dma_start(
@@ -196,7 +198,7 @@ def tile_gcnfast_t_v_kernel(tc, h, e, AA_mask, GCW, GCB, z, grad_out, out):
                 )
 
             for g in range(PASSES):
-                for rows in FIRST_ROWS if g == 0 else [slice(0, PACK)]:
+                for rows in ROW_HALVES:
                     nc.vector.tensor_tensor(
                         out=gcw_tiles[g][:, rows, :],
                         in0=mask_tiles[g][:, rows, :],
@@ -241,15 +243,14 @@ def tile_gcnfast_t_v_kernel(tc, h, e, AA_mask, GCW, GCB, z, grad_out, out):
             for turn in range(TURN_BANKS):
                 turn_back()
             relu_on_scalar(1)
-            quantise_a(1)
             for pair in range(FIRST_PAIRS, PAIRS - GROUP // PAIR):
                 first_turn(pair)
             dz_grouped = new_dz()
             mask_pair(dz_grouped, 0, 0)
-            first_turn(LAST_PAIRS[0])
             mask_pair(dz_grouped, 0, 1)
+            quantise_a(1)
+            first_turn(LAST_PAIRS[0])
             mask_pair(dz_grouped, 1, 0)
-            first_turn(LAST_PAIRS[1])
             mask_pair(dz_grouped, 1, 1)
 
         stores = ctx.enter_context(tc.tile_pool(name="stores", bufs=3))
@@ -295,6 +296,8 @@ def tile_gcnfast_t_v_kernel(tc, h, e, AA_mask, GCW, GCB, z, grad_out, out):
                     for pair in range(group * GROUP // PAIR, (group + 1) * GROUP // PAIR):
                         for g in range(PASSES):
                             mask_pair(dz_grouped, pair, g)
+                        if pair == GROUP // PAIR:
+                            first_turn(LAST_PAIRS[1])
                 for g in range(PASSES):
                     nc.vector.quantize_mx(
                         out=dz_codes[:, g, :].bitcast(E5M2_X4),

@@ -32,6 +32,7 @@ PAIRS = BATCH // PAIR
 QUAD = 4
 BANK_BF16 = 1024
 HALVES = (4, 8)
+LAST_PIECES = (2, 4, 8)
 ROW_HALVES = (slice(0, 2), slice(2, 4))
 SCALAR_COLUMNS = (288, 128)
 FIRST_PAIRS = 2
@@ -152,22 +153,29 @@ def tile_gcnfast_t_v_kernel(tc, h, e, AA_mask, GCW, GCB, z, grad_out, out):
 
             def load_z(pair, pairs):
                 z_t = loads.tile([P, pairs * PAIR, ROWS, FEAT], F32, name="z_%d" % pair)
-                nc.sync.dma_start(
-                    out=z_t[:].rearrange("p b (g u) d -> p (b g) (u d)", u=PACK),
-                    in_=z_rows[:, pair * PAIR * PASSES : (pair + pairs) * PAIR * PASSES, :],
-                )
+                if pair == 1:
+                    for g in range(PASSES):
+                        nc.sync.dma_start(
+                            out=z_t[:, :, g * PACK : (g + 1) * PACK, :].rearrange("p b u d -> p b (u d)"),
+                            in_=z_passes[g][:, pair * PAIR : (pair + 1) * PAIR, :],
+                        )
+                else:
+                    nc.sync.dma_start(
+                        out=z_t[:].rearrange("p b (g u) d -> p (b g) (u d)", u=PACK),
+                        in_=z_rows[:, pair * PAIR * PASSES : (pair + pairs) * PAIR * PASSES, :],
+                    )
                 for q in range(pairs):
                     z_tiles.append(z_t[:, q * PAIR : (q + 1) * PAIR, :, :])
 
-            for pair in range(0, 2 * FIRST_PAIRS, 2):
-                load_g(pair, 2)
+            load_g(0, 2)
             load_z(0, 1)
-            load_g(2 * FIRST_PAIRS, 2)
+            load_g(2, 2)
+            load_g(4, 2)
             load_z(1, 1)
             load_g(LAST_PAIRS[0], 1)
             load_z(2, 1)
-            load_g(LAST_PAIRS[1], 1)
             load_z(3, 1)
+            load_g(LAST_PAIRS[1], 1)
             load_z(4, 1)
             load_z(5, 1)
             for g in range(PASSES):
@@ -341,4 +349,4 @@ def tile_gcnfast_t_v_kernel(tc, h, e, AA_mask, GCW, GCB, z, grad_out, out):
                 for m in range(M_TILES):
                     acc = (early + late)[m]
                     multiply(acc, dz_codes, dz_scales, m, 1)
-                    leave(staged, acc, group, m, HALVES, "vector" if m % 2 == 1 else "scalar")
+                    leave(staged, acc, group, m, LAST_PIECES, "vector" if m % 2 == 1 else "scalar")

from contextlib import ExitStack

import concourse.masks as masks
import concourse.mybir as mybir

F32 = mybir.dt.float32
BF16 = mybir.dt.bfloat16
U32 = mybir.dt.uint32
U8 = mybir.dt.uint8
E4M3_X4 = mybir.dt.float8_e4m3fn_x4
E5M2_X4 = mybir.dt.float8_e5m2_x4
ALU = mybir.AluOpType

P = 128
PACK = 4
K_PASS = P * PACK

BATCH, NODES, STEPS, FEAT = 16, 64, 16, 128
I = STEPS * NODES
J = STEPS * NODES
PASSES = I // K_PASS
ROWS = I // P
QUARTETS = NODES // PACK

N_TILE = 512
GROUP = N_TILE // FEAT
GROUPS = BATCH // GROUP
M_TILES = J // P
HALF_STEPS = STEPS // 2
PAIR = P // NODES
PAIRS = BATCH // PAIR
QUAD = 4
BANK_BF16 = 1024
HALVES = (4, 8)
LAST_PIECES = (2, 4, 8)
ROW_HALVES = (slice(0, 2), slice(2, 4))
SCALAR_COLUMNS = (288, 128)
FIRST_PAIRS = 2
TURN_BANKS = 4
LAST_PAIRS = range(PAIRS - GROUP // PAIR, PAIRS)
TURN_ORDER = [(pair, g) for pair in range(PAIRS - GROUP // PAIR) for g in range(PASSES)] + [
    (pair, g) for g in range(PASSES) for pair in LAST_PAIRS
]

FLOPS = 2 * I * J * BATCH * FEAT
BYTES = 2 * (2 * I * J) + 4 * BATCH * I * FEAT + 2 * BATCH * I * FEAT + 4 * BATCH * J * FEAT


def tile_gcnfast_t_v_kernel(tc, h, e, AA_mask, GCW, GCB, z, grad_out, out):
    nc = tc.nc

    mask_rows = AA_mask.rearrange("(g p u) j -> g p (u j)", p=P, u=PACK)
    gcw_rows = GCW.rearrange("(g p u) j -> g p (u j)", p=P, u=PACK)
    z_rows = z.rearrange("b (g p u) d -> p (b g) (u d)", p=P, u=PACK)
    z_passes = z.rearrange("b (g p u) d -> g p b (u d)", p=P, u=PACK)
    g_pairs = grad_out.rearrange("(pair bl) s t d -> (bl s) pair (t d)", bl=PAIR)
    out_rows = out.rearrange("b c t d -> b (c t d)").rearrange("b (q r) -> q b r", q=P)

    with ExitStack() as ctx:
        keep = ctx.enter_context(tc.tile_pool(name="keep", bufs=1))
        loads = ctx.enter_context(tc.tile_pool(name="loads", bufs=1))
        quant = ctx.enter_context(tc.tile_pool(name="quant", bufs=2))
        turn_psum = ctx.enter_context(tc.psum_pool(name="turn_psum", bufs=TURN_BANKS))
        psum = ctx.enter_context(tc.psum_pool(name="psum", bufs=8 - TURN_BANKS))
        ctx.enter_context(tc.manual_schedule())

        ident = keep.tile([P, P], BF16)
        masks.make_identity(nc, ident[:])
        ident_words = keep.tile([P, P], F32)
        masks.make_identity(nc, ident_words[:])
        sorter = keep.tile([P, P], BF16)
        nc.vector.tensor_copy(
            out=sorter[:].rearrange("i (u s4 bl) -> i u s4 bl", u=PACK, bl=PAIR),
            in_=ident[:].rearrange("i (bl s4 u) -> i u s4 bl", u=PACK, bl=PAIR),
        )
        warm = keep.tile([P, 1], F32)
        nc.scalar.activation(out=warm[:], in_=ident_words[:, 0:1], func=mybir.ActivationFunctionType.Relu)
        a_grouped = keep.tile([P, PASSES, J * PACK], BF16, align_bytes=64)
        a_codes = keep.tile([P, PASSES, J], U32, align_bytes=64)
        a_scales = keep.tile([P, PASSES, J], U8, align_bytes=64)
        by_feature = keep.tile([P, PASSES, PAIRS, PACK, P, PAIR], BF16)

        g_banks = {}

        def turn_back():
            pair, g = TURN_ORDER[len(g_banks)]
            bank_back = turn_psum.tile([P, PACK, FEAT], F32, tag="turn")
            for u in range(PACK):
                nc.tensor.transpose(
                    out=bank_back[:, u, :],
                    in_=by_feature[:, g, pair, u, :, :].rearrange("d p bl -> d (p bl)").bitcast(F32),
                    identity=ident_words[:],
                )
            g_banks[(pair, g)] = bank_back

        z_tiles = []
        last_z = []

        def new_dz():
            return quant.tile([P, PASSES, GROUP, FEAT, PACK], BF16, align_bytes=64, name="dz_grouped")

        def mask_pair(dz_grouped, pair, g):
            rows = slice(g * PACK, (g + 1) * PACK)
            turned = (
                g_banks[(pair, g)][:]
                .rearrange("p u d -> p (u d)")
                .bitcast(BF16)
                .rearrange("p (u d bl) -> p bl d u", u=PACK, bl=PAIR)
            )
            for bl in range(PAIR):
                place = (pair * PAIR + bl) % GROUP
                z_block = last_z[g][:, place, :, :] if pair in LAST_PAIRS else z_tiles[pair][:, bl, rows, :]
                nc.vector.scalar_tensor_tensor(
                    out=dz_grouped[:, g, place, :, :],
                    in0=z_block.rearrange("p u d -> p d u"),
                    scalar=0.0,
                    in1=turned[:, bl, :, :],
                    op0=ALU.is_gt,
                    op1=ALU.mult,
                )
            if len(g_banks) < len(TURN_ORDER):
                turn_back()

        with ExitStack() as head:
            weights = head.enter_context(tc.tile_pool(name="weights", bufs=PASSES))
            as_it_lies = head.enter_context(tc.tile_pool(name="as_it_lies", bufs=1))

            mask_tiles = []
            gcw_tiles = []
            for g in range(PASSES):
                mask_t = weights.tile([P, PACK, J], BF16)
                gcw_t = weights.tile([P, PACK, J], BF16)
                for rows in ROW_HALVES:
                    run = slice(rows.start * J, rows.stop * J)
                    nc.sync.dma_start(
                        out=mask_t[:, rows, :].rearrange("p u j -> p (u j)"), in_=mask_rows[g][:, run]
                    )
                    nc.sync.dma_start(
                        out=gcw_t[:, rows, :].rearrange("p u j -> p (u j)"), in_=gcw_rows[g][:, run]
                    )
                mask_tiles.append(mask_t)
                gcw_tiles.append(gcw_t)
            g_tiles = []

            def load_g(pair, pairs):
                pool = loads if pair == LAST_PAIRS[1] else as_it_lies
                g_t = pool.tile([P, pairs, STEPS, FEAT], BF16, name="grad_%d" % pair)
                nc.sync.dma_start(
                    out=g_t[:].rearrange("p q t d -> p q (t d)"), in_=g_pairs[:, pair : pair + pairs, :]
                )
                for q in range(pairs):
                    g_tiles.append(g_t[:, q, :, :])

            def load_z(pair, pairs):
                z_t = loads.tile([P, pairs * PAIR, ROWS, FEAT], F32, name="z_%d" % pair)
                if pair == 1:
                    for g in range(PASSES):
                        nc.sync.dma_start(
                            out=z_t[:, :, g * PACK : (g + 1) * PACK, :].rearrange("p b u d -> p b (u d)"),
                            in_=z_passes[g][:, pair * PAIR : (pair + 1) * PAIR, :],
                        )
                else:
                    nc.sync.dma_start(
                        out=z_t[:].rearrange("p b (g u) d -> p (b g) (u d)", u=PACK),
                        in_=z_rows[:, pair * PAIR * PASSES : (pair + pairs) * PAIR * PASSES, :],
                    )
                for q in range(pairs):
                    z_tiles.append(z_t[:, q * PAIR : (q + 1) * PAIR, :, :])

            load_g(0, 2)
            load_z(0, 1)
            load_g(2, 2)
            load_g(4, 2)
            load_z(1, 1)
            load_g(LAST_PAIRS[0], 1)
            load_z(2, 1)
            load_z(3, 1)
            load_g(LAST_PAIRS[1], 1)
            load_z(4, 1)
            load_z(5, 1)
            for g in range(PASSES):
                z_t = loads.tile([P, GROUP, PACK, FEAT], F32, name="last_z_%d" % g)
                nc.sync.dma_start(
                    out=z_t[:].rearrange("p b u d -> p b (u d)"), in_=z_passes[g][:, BATCH - GROUP :, :]
                )
                last_z.append(z_t)

            def grouped_view(g):
                return a_grouped[:, g, :].rearrange("p (mc th u) -> p mc th u", th=2, u=PACK)

            def product_view(g):
                return gcw_tiles[g][:].rearrange("p u (th mc) -> p mc th u", th=2)

            def relu_on_scalar(g):
                nc.scalar.activation(
                    out=grouped_view(g)[:, : SCALAR_COLUMNS[g], :, :],
                    in_=product_view(g)[:, : SCALAR_COLUMNS[g], :, :],
                    func=mybir.ActivationFunctionType.Relu,
                )

            def quantise_a(g):
                nc.vector.quantize_mx(
                    out=a_codes[:, g, :].bitcast(E4M3_X4),
                    scales=a_scales[:, g, :],
                    in_=a_grouped[:, g, :],
                )

            for g in range(PASSES):
                for rows in ROW_HALVES:
                    nc.vector.tensor_tensor(
                        out=gcw_tiles[g][:, rows, :],
                        in0=mask_tiles[g][:, rows, :],
                        in1=gcw_tiles[g][:, rows, :],
                        op=ALU.mult,
                    )
                if g == 0:
                    relu_on_scalar(g)
                nc.vector.tensor_scalar_max(
                    out=grouped_view(g)[:, SCALAR_COLUMNS[g] :, :, :],
                    in0=product_view(g)[:, SCALAR_COLUMNS[g] :, :, :],
                    scalar1=0.0,
                )
            quantise_a(0)

            def first_turn(pair):
                for quad in range(STEPS // QUAD):
                    bank_in = psum.tile([P, BANK_BF16], BF16, tag="acc")
                    for k in range(QUAD):
                        nc.tensor.transpose(
                            out=bank_in[:, k * P : (k + 1) * P],
                            in_=g_tiles[pair][:, quad * QUAD + k, :],
                            identity=sorter[:],
                        )
                    g = quad * QUAD // HALF_STEPS
                    first_p = (quad * QUAD % HALF_STEPS) * QUARTETS
                    nc.scalar.copy(
                        out=by_feature[:, g, pair, :, :, :]
                        .rearrange("d u p bl -> d (u p bl)")
                        .bitcast(F32)
                        .rearrange("d (u p) -> d u p", p=P)[
                            :, :, first_p : first_p + QUAD * QUARTETS
                        ]
                        .rearrange("d u (k s4) -> d u k s4", k=QUAD),
                        in_=bank_in[:, : QUAD * P]
                        .bitcast(F32)
                        .rearrange("d (k u s4) -> d u k s4", k=QUAD, s4=QUARTETS),
                    )

            for pair in range(FIRST_PAIRS):
                first_turn(pair)
            for turn in range(TURN_BANKS):
                turn_back()
            relu_on_scalar(1)
            for pair in range(FIRST_PAIRS, PAIRS - GROUP // PAIR):
                first_turn(pair)
            dz_grouped = new_dz()
            mask_pair(dz_grouped, 0, 0)
            mask_pair(dz_grouped, 0, 1)
            quantise_a(1)
            first_turn(LAST_PAIRS[0])
            mask_pair(dz_grouped, 1, 0)
            mask_pair(dz_grouped, 1, 1)

        stores = ctx.enter_context(tc.tile_pool(name="stores", bufs=3))
        def multiply(acc, dz_codes, dz_scales, m, g):
            cols = slice(m * P, (m + 1) * P)
            nc.tensor.matmul_mx(
                out=acc[:],
                lhsT=a_codes[:, g, cols].bitcast(E4M3_X4),
                lhsT_scale=a_scales[:, g, cols],
                rhs=dz_codes[:, g, :].bitcast(E5M2_X4),
                rhs_scale=dz_scales[:, g, :],
                start=(g == 0),
                stop=(g == PASSES - 1),
            )

        def leave(staged, acc, group, m, pieces, engine):
            if engine == "vector":
                nc.vector.tensor_copy(
                    out=staged[:, :, m, :], in_=acc[:].rearrange("p (b d) -> p b d", b=GROUP)
                )
            else:
                nc.scalar.copy(
                    out=staged[:, :, m, :], in_=acc[:].rearrange("p (b d) -> p b d", b=GROUP)
                )
            if m + 1 in pieces:
                first_m = ([0] + list(pieces))[pieces.index(m + 1)]
                nc.sync.dma_start(
                    out=out_rows[
                        :, group * GROUP : (group + 1) * GROUP, first_m * FEAT : (m + 1) * FEAT
                    ],
                    in_=staged[:, :, first_m : m + 1, :].rearrange("p b t d -> p b (t d)"),
                )

        for group in range(GROUPS):
            last = group == GROUPS - 1
            if group > 0:
                dz_grouped = new_dz()
            dz_codes = quant.tile([P, PASSES, N_TILE], U32, align_bytes=64)
            dz_scales = quant.tile([P, PASSES, N_TILE], U8, align_bytes=64)
            staged = stores.tile([P, GROUP, HALF_STEPS, FEAT], F32)
            if not last:
                if group > 0:
                    for pair in range(group * GROUP // PAIR, (group + 1) * GROUP // PAIR):
                        for g in range(PASSES):
                            mask_pair(dz_grouped, pair, g)
                        if pair == GROUP // PAIR:
                            first_turn(LAST_PAIRS[1])
                for g in range(PASSES):
                    nc.vector.quantize_mx(
                        out=dz_codes[:, g, :].bitcast(E5M2_X4),
                        scales=dz_scales[:, g, :],
                        in_=dz_grouped[:, g, :, :, :].rearrange("p b d u -> p (b d u)"),
                    )
                for m in range(M_TILES):
                    acc = psum.tile([P, N_TILE], F32, tag="acc")
                    for g in range(PASSES):
                        multiply(acc, dz_codes, dz_scales, m, g)
                    leave(staged, acc, group, m, HALVES if group == GROUPS - 2 else (M_TILES,), "scalar")
            else:
                early = []
                late = []

                def open_late():
                    acc = turn_psum.tile([P, N_TILE], F32, tag="turn")
                    multiply(acc, dz_codes, dz_scales, len(early) + len(late), 0)
                    late.append(acc)

                for g in range(PASSES):
                    for pair in range(PAIRS - GROUP // PAIR, PAIRS):
                        mask_pair(dz_grouped, pair, g)
                        if g == PASSES - 1:
                            open_late()
                    for half in range(2):
                        batches = slice(half * PAIR, (half + 1) * PAIR)
                        columns = slice(half * PAIR * FEAT, (half + 1) * PAIR * FEAT)
                        nc.vector.quantize_mx(
                            out=dz_codes[:, g, columns].bitcast(E5M2_X4),
                            scales=dz_scales[:, g, columns],
                            in_=dz_grouped[:, g, batches, :, :].rearrange("p b d u -> p (b d u)"),
                        )
                    if g == 0:
                        for m in range(8 - TURN_BANKS):
                            acc = psum.tile([P, N_TILE], F32, tag="acc")
                            multiply(acc, dz_codes, dz_scales, m, 0)
                            early.append(acc)
                        for pair in range(GROUP // PAIR):
                            open_late()
                for m in range(M_TILES):
                    acc = (early + late)[m]
                    multiply(acc, dz_codes, dz_scales, m, 1)
                    leave(staged, acc, group, m, LAST_PIECES, "vector" if m % 2 == 1 else "scalar")
